import numpy as np
import ml_dtypes


def mxq(x, axis, fmt="e4m3"):
    dtype, down = {"e4m3": (ml_dtypes.float8_e4m3fn, 7), "e5m2": (ml_dtypes.float8_e5m2, 14)}[fmt]
    v = np.moveaxis(np.asarray(x, np.float32).astype(ml_dtypes.bfloat16).astype(np.float64), axis, -1)
    blocks = v.reshape(v.shape[:-1] + (-1, 32))
    amax = np.abs(blocks).max(-1, keepdims=True)
    byte = np.maximum(np.where(amax > 0, np.frexp(amax)[1] - 1 + 127, 0) - down, 1)
    scale = np.exp2(byte - 127.0)
    codes = (blocks / scale).astype(np.float32).astype(dtype).astype(np.float64)
    return np.moveaxis((codes * scale).reshape(v.shape), -1, axis)


WIDE = False


def mx_kscale(k):
    if not WIDE:
        return np.ones(k)
    levels = np.array([10, -10, 5, -5, 0])
    if k % 512:
        return np.exp2(np.random.permutation(np.resize(levels, k // 32))).repeat(32)
    a = np.empty((k // 512, 16))
    for p in range(k // 512):
        a[p, :8] = np.random.permutation(np.resize(levels, 8))
        for g in range(8):
            far = levels[np.abs(levels - a[p, g]) >= 10]
            a[p, g + 8] = far[np.random.randint(len(far))]
    return np.exp2(a.ravel()).repeat(32)


BF16 = ml_dtypes.bfloat16


def bf(x):
    return np.asarray(x, np.float32).astype(BF16)


def f64(x):
    return np.asarray(x).astype(np.float64)


BS, DIN, MID, OUT = 1024, 512, 1024, 512
D1, D2, K = 2, 4, 2
EPS = 1e-5


def dilated_nodes(queue, dilation, new_node):
    nodes = np.concatenate([queue[0::dilation], new_node[None]], axis=0)
    bs = new_node.shape[0]
    return np.moveaxis(nodes[..., 0], 0, -1).reshape(bs, -1)


def bn_eval(h, scale, bias, mean, var):
    return (h - mean) * (scale * (1.0 / np.sqrt(var + EPS))) + bias


def setup_inputs():
    s = mx_kscale(DIN * K).reshape(DIN, K)
    t = mx_kscale(MID * K).reshape(MID, K)
    qs1 = np.repeat(s[:, :K - 1].T, D1, axis=0)[:, None, :, None]
    qs2 = np.repeat(t[:, :K - 1].T, D2, axis=0)[:, None, :, None]
    return {
        "x": bf(np.random.standard_normal((BS, DIN, 1)) * s[None, :, K - 1:]),
        "conv1_queue": bf(np.random.standard_normal((D1 * (K - 1), BS, DIN, 1)) * qs1),
        "conv2_queue": bf(np.random.standard_normal((D2 * (K - 1), BS, MID, 1)) * qs2),
        "w1": bf(np.random.standard_normal((MID, DIN * K)) / np.sqrt(DIN * K) / s.reshape(-1)[None, :]),
        "b1": bf(np.random.standard_normal(MID) * 0.1),
        "w2": bf(np.random.standard_normal((OUT, MID * K)) / np.sqrt(MID * K) / t.reshape(-1)[None, :]),
        "b2": bf(np.random.standard_normal(OUT) * 0.1),
        "w_skip": bf(np.random.standard_normal((OUT, DIN * K)) / np.sqrt(DIN * K) / s.reshape(-1)[None, :]),
        "b_skip": bf(np.random.standard_normal(OUT) * 0.1),
        "bn1_scale": bf(np.random.uniform(0.5, 1.5, MID) * t[:, K - 1]),
        "bn1_bias": bf(np.random.standard_normal(MID) * 0.1 * t[:, K - 1]),
        "bn1_mean": bf(np.random.standard_normal(MID) * 0.1),
        "bn1_var": bf(np.random.uniform(0.5, 1.5, MID)),
        "bn2_scale": bf(np.random.uniform(0.5, 1.5, OUT)),
        "bn2_bias": bf(np.random.standard_normal(OUT) * 0.1),
        "bn2_mean": bf(np.random.standard_normal(OUT) * 0.1),
        "bn2_var": bf(np.random.uniform(0.5, 1.5, OUT)),
    }


def reference(x, conv1_queue, conv2_queue, w1, b1, w2, b2, w_skip, b_skip,
              bn1_scale, bn1_bias, bn1_mean, bn1_var,
              bn2_scale, bn2_bias, bn2_mean, bn2_var):
    l1_input = dilated_nodes(f64(conv1_queue), D1, f64(x))
    l1q = mxq(l1_input, 1, "e4m3")
    conv1_out = (l1q @ mxq(f64(w1), 1, "e4m3").T) + f64(b1)
    conv1_out = bn_eval(np.maximum(conv1_out, 0.0), f64(bn1_scale), f64(bn1_bias), f64(bn1_mean), f64(bn1_var))
    l2_input = dilated_nodes(f64(conv2_queue), D2, conv1_out[:, :, None])
    conv2_out = (mxq(l2_input, 1, "e4m3") @ mxq(f64(w2), 1, "e4m3").T) + f64(b2)
    conv2_out = conv2_out + ((l1q @ mxq(f64(w_skip), 1, "e4m3").T) + f64(b_skip))
    conv2_out = np.maximum(conv2_out, 0.0)
    conv2_out = bn_eval(conv2_out, f64(bn2_scale), f64(bn2_bias), f64(bn2_mean), f64(bn2_var))
    return conv2_out[:, :, None]

@@ -1,0 +1,456 @@
+from contextlib import ExitStack
+
+import concourse.mybir as mybir
+from concourse.masks import make_identity
+
+F32 = mybir.dt.float32
+BF16 = mybir.dt.bfloat16
+U32 = mybir.dt.uint32
+U8 = mybir.dt.uint8
+FP8X4 = mybir.dt.float8_e4m3fn_x4
+ALU = mybir.AluOpType
+ACTF = mybir.ActivationFunctionType
+
+P = 128
+BS, DIN, MID, OUT = 1024, 512, 1024, 512
+EPS = 1e-5
+BIG = 3.0e38
+FLOPS = 2 * BS * (2 * DIN * MID + 2 * MID * OUT + 2 * DIN * OUT)
+BYTES = 2 * (2 * BS * DIN + BS * MID + 2 * DIN * MID + 2 * MID * OUT + 2 * DIN * OUT) + 4 * BS * OUT
+
+MANUAL = False
+CW = ("act", "act", "act", "dve")
+
+
+def tile_autoregressiveresidualblock_kernel(
+    tc, x, conv1_queue, conv2_queue, w1, b1, w2, b2, w_skip, b_skip,
+    bn1_scale, bn1_bias, bn1_mean, bn1_var, bn2_scale, bn2_bias, bn2_mean, bn2_var, out,
+):
+    nc = tc.nc
+    with ExitStack() as ctx:
+        const = ctx.enter_context(tc.tile_pool(name="const", bufs=1))
+        raw = ctx.enter_context(tc.tile_pool(name="raw", bufs=1))
+        keep = ctx.enter_context(tc.tile_pool(name="keep", bufs=1))
+        grp_pool = ctx.enter_context(tc.tile_pool(name="grp", bufs=8))
+        s_pool = ctx.enter_context(tc.tile_pool(name="spool", bufs=8))
+        gg_pool = ctx.enter_context(tc.tile_pool(name="gg", bufs=4))
+        v_pool = ctx.enter_context(tc.tile_pool(name="vpool", bufs=4))
+        o_pool = ctx.enter_context(tc.tile_pool(name="opool", bufs=4))
+        ps_t = ctx.enter_context(tc.psum_pool(name="pst", bufs=4))
+        ps_a = ctx.enter_context(tc.psum_pool(name="psa", bufs=4))
+        if MANUAL:
+            ctx.enter_context(tc.manual_schedule())
+
+        live = {}
+
+        def evac(eng, dst, src):
+            if eng == "act":
+                nc.scalar.copy(out=dst, in_=src)
+            else:
+                nc.vector.tensor_copy(out=dst, in_=src)
+
+        rows1 = const.tile([P, 2 * P], BF16, name="rows1", tag="rows1")
+        rows2 = const.tile([P, P], BF16, name="rows2", tag="rows2")
+        nc.vector.memset(rows1[:], 0.0)
+        for n, vec in enumerate((b1, bn1_scale, bn1_bias, bn1_mean, bn1_var)):
+            nc.scalar.dma_start(out=rows1[4 * n:4 * n + 4, :], in_=vec.rearrange("(i p) -> i p", p=2 * P))
+        ident_b = const.tile([P, P], BF16, name="ident_b", tag="ident_b")
+        nc.vector.memset(ident_b[:], 0.0)
+        make_identity(nc, ident_b[:], nomemset=True)
+        ident_f = const.tile([P, P], F32, name="ident_f", tag="ident_f")
+        nc.vector.tensor_copy(out=ident_f[:], in_=ident_b[:])
+        nc.vector.memset(rows2[:], 0.0)
+        warm = const.tile([P, 1], F32, name="warm", tag="warm")
+        nc.vector.memset(warm[:], 1.0)
+        nc.scalar.activation(out=warm[:], in_=warm[:], func=ACTF.Sqrt)
+
+        def load_rows2():
+            for n, vec in enumerate((b2, b_skip, bn2_scale, bn2_bias, bn2_mean, bn2_var)):
+                nc.sync.dma_start(out=rows2[4 * n:4 * n + 4, :], in_=vec.rearrange("(i p) -> i p", p=P))
+
+        a_sb = raw.tile([P, 2 * 8 * DIN], BF16, name="a_sb", tag="a_sb")
+        q2_sb = raw.tile([P, 8 * MID], BF16, name="q2_sb", tag="q2_sb")
+        w1_sb = raw.tile([P, 8 * 2 * DIN], BF16, name="w1_sb", tag="w1_sb")
+        ws_sb = raw.tile([P, 4 * 2 * DIN], BF16, name="ws_sb", tag="ws_sb")
+        w2_sb = raw.tile([P, 4 * 2 * MID], BF16, name="w2_sb", tag="w2_sb")
+        a_t = a_sb[:].rearrange("p (e t c) -> p e t c", e=2, t=8)
+        taps = (
+            conv1_queue[0].rearrange("(e j t) c o -> j e t (c o)", e=2, t=8),
+            x.rearrange("(e j t) c o -> j e t (c o)", e=2, t=8),
+        )
+        q2_v = conv2_queue[0].rearrange("(p t) c o -> p t (c o)", t=8)
+        q2_t = q2_sb[:].rearrange("p (t c) -> p t c", t=8)
+        w1_v = w1.rearrange("(g p e) k -> p g (e k)", p=P, e=2)
+        ws_v = w_skip.rearrange("(i p) k -> p i k", p=P)
+        w2_v = w2.rearrange("(i p) k -> p i k", p=P)
+        ws_t = ws_sb[:].rearrange("p (i k) -> p i k", i=4)
+        w2_t = w2_sb[:].rearrange("p (i k) -> p i k", i=4)
+
+        def load_a(t0, nt):
+            for tap in range(2):
+                nc.sync.dma_start(out=a_t[tap:P:2, :, t0:t0 + nt, :], in_=taps[tap][:, :, t0:t0 + nt, :])
+
+        def load_w1():
+            for pr in range(4):
+                nc.sync.dma_start(out=w1_sb[:, 4 * DIN * pr:4 * DIN * pr + 4 * DIN], in_=w1_v[:, pr, :])
+
+        def load_q2(h):
+            nc.sync.dma_start(out=q2_t[:, 4 * h:4 * h + 4, :], in_=q2_v[:, 4 * h:4 * h + 4, :])
+
+        def load_ws():
+            nc.sync.dma_start(out=ws_t, in_=ws_v)
+
+        def load_w2():
+            for pr in range(2):
+                nc.sync.dma_start(out=w2_t[:, 2 * pr:2 * pr + 2, :], in_=w2_v[:, 2 * pr:2 * pr + 2, :])
+
+        a_c = keep.tile([P, 2, BS], U32, name="a_c", tag="a_c", align_bytes=64)
+        a_s = keep.tile([P, 2, BS], U8, name="a_s", tag="a_s", align_bytes=64)
+        g_c = keep.tile([P, 4, BS], U32, name="g_c", tag="g_c", align_bytes=64)
+        g_s = keep.tile([P, 4, BS], U8, name="g_s", tag="g_s", align_bytes=64)
+        w1_c = keep.tile([P, 2, MID], U32, name="w1_c", tag="w1_c", align_bytes=64)
+        w1_s = keep.tile([P, 2, MID], U8, name="w1_s", tag="w1_s", align_bytes=64)
+        ws_c = keep.tile([P, 2, OUT], U32, name="ws_c", tag="ws_c", align_bytes=64)
+        ws_s = keep.tile([P, 2, OUT], U8, name="ws_s", tag="ws_s", align_bytes=64)
+        w2_c = keep.tile([P, 4, OUT], U32, name="w2_c", tag="w2_c", align_bytes=64)
+        w2_s = keep.tile([P, 4, OUT], U8, name="w2_s", tag="w2_s", align_bytes=64)
+        weights = {
+            "w1": (w1_sb[:].bitcast(F32), DIN, w1_c, w1_s),
+            "ws": (ws_sb[:].bitcast(F32), DIN, ws_c, ws_s),
+            "w2": (w2_sb[:].bitcast(F32), MID, w2_c, w2_s),
+        }
+
+        vt1 = const.tile([P, 40], F32, name="vt1", tag="vt1")
+        gain1 = const.tile([P, 8], F32, name="gain1", tag="gain1")
+        shift1 = const.tile([P, 8], F32, name="shift1", tag="shift1")
+        bias1 = const.tile([P, 8], F32, name="bias1", tag="bias1")
+        mask1 = const.tile([P, 8], F32, name="mask1", tag="mask1")
+        part1 = const.tile([P, 8], F32, name="part1", tag="part1")
+        lo1 = const.tile([P, 8], F32, name="lo1", tag="lo1")
+        hi1 = const.tile([P, 8], F32, name="hi1", tag="hi1")
+        vt2 = const.tile([P, 24], F32, name="vt2", tag="vt2")
+        gain2 = const.tile([P, 4], F32, name="gain2", tag="gain2")
+        shift2 = const.tile([P, 4], F32, name="shift2", tag="shift2")
+        bias2 = const.tile([P, 4], F32, name="bias2", tag="bias2")
+        mask2 = const.tile([P, 4], F32, name="mask2", tag="mask2")
+        part2 = const.tile([P, 4], F32, name="part2", tag="part2")
+        lo2 = const.tile([P, 4], F32, name="lo2", tag="lo2")
+        hi2 = const.tile([P, 4], F32, name="hi2", tag="hi2")
+        bsum = const.tile([P, 4], F32, name="bsum", tag="bsum")
+
+        def prep_T1():
+            tp = ps_t.tile([P, 2, P], BF16, name="tp", tag="tp")
+            for e in range(2):
+                nc.tensor.transpose(tp[:, e, :], rows1[:, e:2 * P:2], ident_b[:])
+            live["rows1"] = tp
+
+        def prep_T2():
+            tp = ps_t.tile([P, P], BF16, name="tp", tag="tp")
+            nc.tensor.transpose(tp[:], rows2[:], ident_b[:])
+            live["rows2"] = tp
+
+        def prep_vectors(vt, n, gain, shift):
+            nc.vector.tensor_scalar_add(out=gain[:], in0=vt[:, 8 + 3 * n:8 + 4 * n], scalar1=EPS)
+            nc.scalar.activation(out=gain[:], in_=gain[:], func=ACTF.Sqrt)
+            nc.vector.reciprocal(out=gain[:], in_=gain[:])
+            nc.vector.tensor_mul(out=gain[:], in0=vt[:, 8:8 + n], in1=gain[:])
+            nc.vector.tensor_mul(out=shift[:], in0=vt[:, 8 + 2 * n:8 + 3 * n], in1=gain[:])
+            nc.vector.tensor_sub(out=shift[:], in0=vt[:, 8 + n:8 + 2 * n], in1=shift[:])
+
+        def prep_clamp(pre, gain, shift, bias, mask, part, lo, hi):
+            nc.vector.tensor_mul(out=bias[:], in0=pre, in1=gain[:])
+            nc.vector.tensor_add(out=bias[:], in0=bias[:], in1=shift[:])
+            nc.vector.tensor_scalar(out=mask[:], in0=gain[:], scalar1=0.0, scalar2=None, op0=ALU.is_ge)
+            nc.vector.tensor_mul(out=part[:], in0=mask[:], in1=shift[:])
+            nc.vector.tensor_scalar(out=lo[:], in0=mask[:], scalar1=-1.0, scalar2=BIG, op0=ALU.add, op1=ALU.mult)
+            nc.vector.tensor_add(out=lo[:], in0=lo[:], in1=part[:])
+            nc.vector.tensor_sub(out=part[:], in0=shift[:], in1=part[:])
+            nc.vector.scalar_tensor_tensor(out=hi[:], in0=mask[:], scalar=BIG, in1=part[:], op0=ALU.mult, op1=ALU.add)
+
+        def prep_bn1():
+            nc.vector.tensor_copy(out=vt1[:].rearrange("p (m e) -> p e m", e=2), in_=live["rows1"][:, :, 0:20])
+            prep_vectors(vt1, 8, gain1, shift1)
+            prep_clamp(vt1[:, 0:8], gain1, shift1, bias1, mask1, part1, lo1, hi1)
+
+        def prep_bn2():
+            nc.vector.tensor_copy(out=vt2[:], in_=live["rows2"][:, 0:24])
+            prep_vectors(vt2, 4, gain2, shift2)
+            nc.vector.tensor_add(out=bsum[:], in0=vt2[:, 0:4], in1=vt2[:, 4:8])
+            prep_clamp(bsum[:], gain2, shift2, bias2, mask2, part2, lo2, hi2)
+
+        def a_T(g, jj):
+            tp = ps_t.tile([P, 1024], BF16, name="tp", tag="tp")
+            for u in range(2):
+                for blk in range(4):
+                    c0 = 512 * u + P * blk
+                    nc.tensor.transpose(tp[:, c0:c0 + P], a_t[:, blk % 2, 2 * jj + blk // 2, 256 * g + u:256 * g + 256:2], ident_b[:])
+            live["aT", g, jj] = tp
+
+        def a_C(g, jj, eng):
+            grp = grp_pool.tile([P, 1024], BF16, name="grp", tag="grp", align_bytes=64)
+            evac(eng, grp[:].bitcast(F32).rearrange("p (n u) -> p n u", u=2),
+                 live["aT", g, jj][:].bitcast(F32).rearrange("p (u n) -> p n u", u=2))
+            live["aC", g, jj] = grp
+
+        def a_Q(g, jj):
+            cols = slice(256 * jj, 256 * jj + 256)
+            nc.vector.quantize_mx(out=a_c[:, g, cols].bitcast(FP8X4), scales=a_s[:, g, cols], in_=live["aC", g, jj][:])
+
+        def w_T(nm, g, j):
+            wf, kw = weights[nm][0], weights[nm][1]
+            tp = ps_t.tile([P, 2, 256], F32, name="tp", tag="tp")
+            for ii in range(2):
+                for u in range(2):
+                    c0 = (2 * j + ii) * kw + 256 * g
+                    nc.tensor.transpose(tp[:, u, P * ii:P * ii + P], wf[:, c0 + u:c0 + 256:2], ident_f[:])
+            live["wT", nm, g, j] = tp
+
+        def w_C(nm, g, j, eng):
+            grp = grp_pool.tile([P, 1024], BF16, name="grp", tag="grp", align_bytes=64)
+            evac(eng, grp[:].bitcast(F32).rearrange("p (r u) -> p r u", u=2), live["wT", nm, g, j][:].rearrange("p u r -> p r u"))
+            live["wC", nm, g, j] = grp
+
+        def w_Q(nm, g, j):
+            cols = slice(256 * j, 256 * j + 256)
+            nc.vector.quantize_mx(out=weights[nm][2][:, g, cols].bitcast(FP8X4), scales=weights[nm][3][:, g, cols], in_=live["wC", nm, g, j][:])
+
+        def s_tile(G, h):
+            if ("S", G, h) not in live:
+                live["S", G, h] = s_pool.tile([P, 4, 512], BF16, name="stile", tag="stile")
+            return live["S", G, h]
+
+        def q_T(G, h):
+            tp = ps_t.tile([P, 2, 512], BF16, name="tp", tag="tp")
+            for u in range(2):
+                for tt in range(4):
+                    nc.tensor.transpose(tp[:, u, P * tt:P * tt + P], q2_t[:, 4 * h + tt, 256 * G + u:256 * G + 256:2], ident_b[:])
+            live["qT", G, h] = tp
+
+        def q_C(G, h, eng):
+            evac(eng, s_tile(G, h)[:, 0:4:2, :], live["qT", G, h][:])
+
+        def l1_M(i, h):
+            acc = ps_a.tile([P, 512], F32, name="acc", tag="acc")
+            for g in range(2):
+                nc.tensor.matmul_mx(
+                    out=acc[:],
+                    lhsT=w1_c[:, g, P * i:P * i + P].bitcast(FP8X4), lhsT_scale=w1_s[:, g, P * i:P * i + P],
+                    rhs=a_c[:, g, 512 * h:512 * h + 512].bitcast(FP8X4), rhs_scale=a_s[:, g, 512 * h:512 * h + 512],
+                    start=(g == 0), stop=(g == 1),
+                )
+            live["l1", i, h] = acc
+
+        def l1_E(i, h):
+            v = v_pool.tile([P, 512], BF16, name="vlin", tag="vlin")
+            nc.scalar.activation(out=v[:], in_=live["l1", i, h][:], func=ACTF.Identity, bias=bias1[:, i:i + 1], scale=gain1[:, i:i + 1])
+            live["v", i, h] = v
+
+        def l1_A(i, h):
+            nc.vector.tensor_scalar(
+                out=s_tile(i // 2, h)[:, 2 * (i % 2) + 1, :], in0=live["v", i, h][:],
+                scalar1=lo1[:, i:i + 1], scalar2=hi1[:, i:i + 1], op0=ALU.max, op1=ALU.min,
+            )
+
+        def g_R(G, h, eng="dve"):
+            gg = gg_pool.tile([P, 2048], BF16, name="ggt", tag="ggt", align_bytes=64)
+            evac(eng, gg[:].rearrange("p (c i t) -> p c t i", i=4, t=4), live["S", G, h][:].rearrange("p t (c i) -> p c t i", i=4))
+            live["gg", G, h] = gg
+
+        def g_Q(G, h):
+            cols = slice(512 * h, 512 * h + 512)
+            nc.vector.quantize_mx(out=g_c[:, G, cols].bitcast(FP8X4), scales=g_s[:, G, cols], in_=live["gg", G, h][:])
+
+        def l2o_M(oi, h, parts):
+            if ("l2o", oi, h) not in live:
+                live["l2o", oi, h] = ps_a.tile([P, 512], F32, name="acc", tag="acc")
+            acc = live["l2o", oi, h]
+            rows = slice(P * oi, P * oi + P)
+            cols = slice(512 * h, 512 * h + 512)
+            for part in parts:
+                if part < 2:
+                    lc, ls, rc, rs, g = ws_c, ws_s, a_c, a_s, part
+                else:
+                    lc, ls, rc, rs, g = w2_c, w2_s, g_c, g_s, part - 2
+                nc.tensor.matmul_mx(
+                    out=acc[:],
+                    lhsT=lc[:, g, rows].bitcast(FP8X4), lhsT_scale=ls[:, g, rows],
+                    rhs=rc[:, g, cols].bitcast(FP8X4), rhs_scale=rs[:, g, cols],
+                    start=(part == 0), stop=(part == 5),
+                )
+
+        def l2o_E(oi, h):
+            v = o_pool.tile([P, 512], F32, name="olin", tag="olin")
+            nc.scalar.activation(out=v[:], in_=live["l2o", oi, h][:], func=ACTF.Identity, bias=bias2[:, oi:oi + 1], scale=gain2[:, oi:oi + 1])
+            live["ov", oi, h] = v
+
+        def l2o_A(oi, h):
+            y = o_pool.tile([P, 512], F32, name="ocl", tag="ocl", align_bytes=64)
+            nc.vector.tensor_scalar(out=y[:], in0=live["ov", oi, h][:], scalar1=lo2[:, oi:oi + 1], scalar2=hi2[:, oi:oi + 1], op0=ALU.max, op1=ALU.min)
+            live["oy", oi, h] = y
+
+        out_r = out.rearrange("(m t) c o -> m t (c o)", t=8)
+
+        def l2o_T(oi, h):
+            tp = ps_t.tile([P, 4, P], F32, name="tp", tag="tp")
+            for tt in range(4):
+                nc.tensor.transpose(tp[:, tt, :], live["oy", oi, h][:, P * tt:P * tt + P], ident_f[:])
+            live["oT", oi, h] = tp
+
+        def l2o_S(oi, h, eng):
+            yt = o_pool.tile([P, 4, P], F32, name="otr", tag="otr")
+            evac(eng, yt[:], live["oT", oi, h][:])
+            nc.sync.dma_start(out=out_r[:, 4 * h:4 * h + 4, P * oi:P * oi + P], in_=yt[:])
+
+        gj = ((0, 0), (1, 0), (0, 1), (1, 1))
+
+        def T(u):
+            if u[0] == "a":
+                a_T(u[1], u[2])
+            elif u[0] == "w":
+                w_T(u[1], u[2], u[3])
+            else:
+                q_T(u[1], u[2])
+
+        def C(u, eng):
+            if u[0] == "a":
+                a_C(u[1], u[2], eng)
+            elif u[0] == "w":
+                w_C(u[1], u[2], u[3], eng)
+            else:
+                q_C(u[1], u[2], eng)
+
+        def Q(u):
+            if u[0] == "a":
+                a_Q(u[1], u[2])
+            elif u[0] == "w":
+                w_Q(u[1], u[2], u[3])
+
+        def t_run(units, engs):
+            for u, e in zip(units, engs):
+                T(u)
+                C(u, e)
+
+        def q_run(units):
+            for u in units:
+                Q(u)
+
+        def l1_run(ms, h):
+            for i in ms:
+                l1_M(i, h)
+                l1_E(i, h)
+
+        def clamps(ms, h):
+            for i in ms:
+                l1_A(i, h)
+
+        def ua(h):
+            return [("a", g, 2 * h + j) for j, g in gj]
+
+        def uw(nm, lst):
+            return [("w", nm, g, j) for g, j in lst]
+
+        def uq(h):
+            return [("q", G, h) for G in range(4)]
+
+        AD = ("act", "dve", "act", "dve")
+        AA = ("act", "act", "act", "act")
+
+        def l2o_fin(oi, h):
+            l2o_E(oi, h)
+            l2o_A(oi, h)
+
+        load_a(0, 2)
+        load_a(2, 2)
+        load_w1()
+        load_a(4, 4)
+        load_q2(0)
+        load_ws()
+        load_w2()
+        load_q2(1)
+        load_rows2()
+
+        def w4(nm, lst):
+            return uw(nm, lst)
+
+        A0 = ua(0)
+        A1 = ua(1)
+        W1a = w4("w1", ((0, 0), (1, 0), (0, 1), (1, 1)))
+        W1b = w4("w1", ((0, 2), (1, 2), (0, 3), (1, 3)))
+        WS = w4("ws", ((0, 0), (0, 1), (1, 0), (1, 1)))
+        W2a = w4("w2", ((0, 0), (0, 1), (1, 0), (1, 1)))
+        W2b = w4("w2", ((2, 0), (2, 1), (3, 0), (3, 1)))
+        Q0 = uq(0)
+        Q1 = uq(1)
+
+        t_run(A0[0:2], AD)
+        t_run(A0[2:4], AD)
+        q_run(A0)
+        t_run(W1a, AD)
+        prep_T1()
+        q_run(W1a)
+        prep_bn1()
+        l1_run((0, 1), 0)
+        t_run(W1b, AD)
+        q_run(W1b)
+        clamps((0, 1), 0)
+        l1_run((2, 3), 0)
+        t_run(A1[0:2], AD)
+        q_run(A1[0:2])
+        clamps((2, 3), 0)
+        l1_run((4, 5), 0)
+        t_run(A1[2:4], AD)
+        q_run(A1[2:4])
+        clamps((4, 5), 0)
+        l1_run((6, 7), 0)
+        t_run(Q0[0:2], AA)
+        clamps((6, 7), 0)
+        g_R(0, 0)
+        l1_run((0, 1), 1)
+        t_run(Q0[2:4], AA)
+        g_R(1, 0)
+        g_Q(0, 0)
+        clamps((0, 1), 1)
+        g_Q(1, 0)
+        l1_run((2, 3), 1)
+        t_run(WS, CW)
+        g_R(2, 0)
+        q_run(WS)
+        clamps((2, 3), 1)
+        g_R(3, 0)
+        g_Q(2, 0)
+        l1_run((4, 5), 1)
+        t_run(W2a, CW)
+        g_Q(3, 0)
+        q_run(W2a)
+        clamps((4, 5), 1)
+        l1_run((6, 7), 1)
+        t_run(W2b, CW)
+        q_run(W2b)
+        clamps((6, 7), 1)
+        l2o_M(0, 0, (0, 1))
+        l2o_M(1, 0, (0, 1))
+        t_run(Q1[0:2], AA)
+        prep_T2()
+        prep_bn2()
+        g_R(0, 1)
+        l2o_M(2, 0, (0, 1))
+        l2o_M(3, 0, (0, 1))
+        t_run(Q1[2:4], AA)
+        groups = [(oi, 0) for oi in range(4)] + [(oi, 1) for oi in range(4)]
+
+        def out_T(ks):
+            for k in ks:
+                l2o_T(groups[k][0], groups[k][1])
+                l2o_S(groups[k][0], groups[k][1], ("act", "dve")[k % 2])
+
+        for n, (oi, h) in enumerate(groups):
+            l2o_M(oi, h, (2, 3, 4, 5) if h == 0 else (0, 1, 2, 3, 4, 5))
+            l2o_E(oi, h)
+            if h == 0:
+                if oi < 3:
+                    g_R(oi + 1, 1)
+                g_Q(oi, 1)
+            l2o_A(oi, h)
+            if n % 2 == 1 and n >= 3:
+                out_T((n - 3, n - 2))
+        out_T((6, 7))

@@ -68,12 +68,13 @@ def tile_autoregressiveresidualblock_kernel(
             for n, vec in enumerate((b2, b_skip, bn2_scale, bn2_bias, bn2_mean, bn2_var)):
                 nc.sync.dma_start(out=rows2[4 * n:4 * n + 4, :], in_=vec.rearrange("(i p) -> i p", p=P))
 
-        a_sb = raw.tile([P, 2 * 8 * DIN], BF16, name="a_sb", tag="a_sb")
+        a_chunks = ((0, 2), (2, 2), (4, 4))
+        a_sb = [raw.tile([P, 2, nt, DIN], BF16, name=f"a_sb{t0}", tag=f"a_sb{t0}") for t0, nt in a_chunks]
         q2_sb = raw.tile([P, 8 * MID], BF16, name="q2_sb", tag="q2_sb")
         w1_sb = raw.tile([P, 8 * 2 * DIN], BF16, name="w1_sb", tag="w1_sb")
         ws_sb = raw.tile([P, 4 * 2 * DIN], BF16, name="ws_sb", tag="ws_sb")
         w2_sb = raw.tile([P, 4 * 2 * MID], BF16, name="w2_sb", tag="w2_sb")
-        a_t = a_sb[:].rearrange("p (e t c) -> p e t c", e=2, t=8)
+        a_of = {t0 + k: (tile, k) for (t0, nt), tile in zip(a_chunks, a_sb) for k in range(nt)}
         taps = (
             conv1_queue[0].rearrange("(e j t) c o -> j e t (c o)", e=2, t=8),
             x.rearrange("(e j t) c o -> j e t (c o)", e=2, t=8),
@@ -86,9 +87,10 @@ def tile_autoregressiveresidualblock_kernel(
         ws_t = ws_sb[:].rearrange("p (i k) -> p i k", i=4)
         w2_t = w2_sb[:].rearrange("p (i k) -> p i k", i=4)
 
-        def load_a(t0, nt):
+        def load_a(n):
+            t0, nt = a_chunks[n]
             for tap in range(2):
-                nc.sync.dma_start(out=a_t[tap:P:2, :, t0:t0 + nt, :], in_=taps[tap][:, :, t0:t0 + nt, :])
+                nc.sync.dma_start(out=a_sb[n][tap:P:2, :, :, :], in_=taps[tap][:, :, t0:t0 + nt, :])
 
         def load_w1():
             for pr in range(4):
@@ -183,7 +185,8 @@ def tile_autoregressiveresidualblock_kernel(
             for u in range(2):
                 for blk in range(4):
                     c0 = 512 * u + P * blk
-                    nc.tensor.transpose(tp[:, c0:c0 + P], a_t[:, blk % 2, 2 * jj + blk // 2, 256 * g + u:256 * g + 256:2], ident_b[:])
+                    src, t = a_of[2 * jj + blk // 2]
+                    nc.tensor.transpose(tp[:, c0:c0 + P], src[:, blk % 2, t, 256 * g + u:256 * g + 256:2], ident_b[:])
             live["aT", g, jj] = tp
 
         def a_C(g, jj, eng):
@@ -359,10 +362,10 @@ def tile_autoregressiveresidualblock_kernel(
             l2o_E(oi, h)
             l2o_A(oi, h)
 
-        load_a(0, 2)
-        load_a(2, 2)
+        load_a(0)
+        load_a(1)
         load_w1()
-        load_a(4, 4)
+        load_a(2)
         load_q2(0)
         load_ws()
         load_w2()

@@ -18,9 +18,6 @@ BIG = 3.0e38
 FLOPS = 2 * BS * (2 * DIN * MID + 2 * MID * OUT + 2 * DIN * OUT)
 BYTES = 2 * (2 * BS * DIN + BS * MID + 2 * DIN * MID + 2 * MID * OUT + 2 * DIN * OUT) + 4 * BS * OUT
 
-MANUAL = False
-CW = ("act", "act", "act", "dve")
-
 
 def tile_autoregressiveresidualblock_kernel(
     tc, x, conv1_queue, conv2_queue, w1, b1, w2, b2, w_skip, b_skip,
@@ -33,13 +30,11 @@ def tile_autoregressiveresidualblock_kernel(
         keep = ctx.enter_context(tc.tile_pool(name="keep", bufs=1))
         grp_pool = ctx.enter_context(tc.tile_pool(name="grp", bufs=8))
         s_pool = ctx.enter_context(tc.tile_pool(name="spool", bufs=8))
-        gg_pool = ctx.enter_context(tc.tile_pool(name="gg", bufs=4))
-        v_pool = ctx.enter_context(tc.tile_pool(name="vpool", bufs=4))
+        gg_pool = ctx.enter_context(tc.tile_pool(name="gg", bufs=5))
+        v_pool = ctx.enter_context(tc.tile_pool(name="vpool", bufs=8))
         o_pool = ctx.enter_context(tc.tile_pool(name="opool", bufs=4))
         ps_t = ctx.enter_context(tc.psum_pool(name="pst", bufs=4))
         ps_a = ctx.enter_context(tc.psum_pool(name="psa", bufs=4))
-        if MANUAL:
-            ctx.enter_context(tc.manual_schedule())
 
         live = {}
 
@@ -52,6 +47,7 @@ def tile_autoregressiveresidualblock_kernel(
         rows1 = const.tile([P, 2 * P], BF16, name="rows1", tag="rows1")
         rows2 = const.tile([P, P], BF16, name="rows2", tag="rows2")
         nc.vector.memset(rows1[:], 0.0)
+        nc.vector.memset(rows2[:], 0.0)
         for n, vec in enumerate((b1, bn1_scale, bn1_bias, bn1_mean, bn1_var)):
             nc.scalar.dma_start(out=rows1[4 * n:4 * n + 4, :], in_=vec.rearrange("(i p) -> i p", p=2 * P))
         ident_b = const.tile([P, P], BF16, name="ident_b", tag="ident_b")
@@ -59,14 +55,9 @@ def tile_autoregressiveresidualblock_kernel(
         make_identity(nc, ident_b[:], nomemset=True)
         ident_f = const.tile([P, P], F32, name="ident_f", tag="ident_f")
         nc.vector.tensor_copy(out=ident_f[:], in_=ident_b[:])
-        nc.vector.memset(rows2[:], 0.0)
         warm = const.tile([P, 1], F32, name="warm", tag="warm")
         nc.vector.memset(warm[:], 1.0)
         nc.scalar.activation(out=warm[:], in_=warm[:], func=ACTF.Sqrt)
-
-        def load_rows2():
-            for n, vec in enumerate((b2, b_skip, bn2_scale, bn2_bias, bn2_mean, bn2_var)):
-                nc.sync.dma_start(out=rows2[4 * n:4 * n + 4, :], in_=vec.rearrange("(i p) -> i p", p=P))
 
         a_chunks = ((0, 2), (2, 2), (4, 4))
         a_sb = [raw.tile([P, 2, nt, DIN], BF16, name=f"a_sb{t0}", tag=f"a_sb{t0}") for t0, nt in a_chunks]
@@ -92,8 +83,8 @@ def tile_autoregressiveresidualblock_kernel(
             for tap in range(2):
                 nc.sync.dma_start(out=a_sb[n][tap:P:2, :, :, :], in_=taps[tap][:, :, t0:t0 + nt, :])
 
-        def load_w1():
-            for pr in range(4):
+        def load_w1(prs):
+            for pr in prs:
                 nc.sync.dma_start(out=w1_sb[:, 4 * DIN * pr:4 * DIN * pr + 4 * DIN], in_=w1_v[:, pr, :])
 
         def load_q2(h):
@@ -101,6 +92,10 @@ def tile_autoregressiveresidualblock_kernel(
 
         def load_ws():
             nc.sync.dma_start(out=ws_t, in_=ws_v)
+
+        def load_rows2():
+            for n, vec in enumerate((b2, b_skip, bn2_scale, bn2_bias, bn2_mean, bn2_var)):
+                nc.sync.dma_start(out=rows2[4 * n:4 * n + 4, :], in_=vec.rearrange("(i p) -> i p", p=P))
 
         def load_w2():
             for pr in range(2):
@@ -138,47 +133,39 @@ def tile_autoregressiveresidualblock_kernel(
         part2 = const.tile([P, 4], F32, name="part2", tag="part2")
         lo2 = const.tile([P, 4], F32, name="lo2", tag="lo2")
         hi2 = const.tile([P, 4], F32, name="hi2", tag="hi2")
-        bsum = const.tile([P, 4], F32, name="bsum", tag="bsum")
 
-        def prep_T1():
-            tp = ps_t.tile([P, 2, P], BF16, name="tp", tag="tp")
-            for e in range(2):
-                nc.tensor.transpose(tp[:, e, :], rows1[:, e:2 * P:2], ident_b[:])
-            live["rows1"] = tp
-
-        def prep_T2():
-            tp = ps_t.tile([P, P], BF16, name="tp", tag="tp")
-            nc.tensor.transpose(tp[:], rows2[:], ident_b[:])
-            live["rows2"] = tp
-
-        def prep_vectors(vt, n, gain, shift):
-            nc.vector.tensor_scalar_add(out=gain[:], in0=vt[:, 8 + 3 * n:8 + 4 * n], scalar1=EPS)
+        def bn_constants(tp_view, vt, vt_view, n, gain, shift, bias, mask, part, lo, hi, two_biases):
+            nc.vector.tensor_copy(out=vt_view, in_=tp_view)
+            nc.gpsimd.tensor_scalar(out=gain[:], in0=vt[:, 8 + 3 * n:8 + 4 * n], scalar1=1.0, scalar2=EPS, op0=ALU.mult, op1=ALU.add)
             nc.scalar.activation(out=gain[:], in_=gain[:], func=ACTF.Sqrt)
             nc.vector.reciprocal(out=gain[:], in_=gain[:])
-            nc.vector.tensor_mul(out=gain[:], in0=vt[:, 8:8 + n], in1=gain[:])
-            nc.vector.tensor_mul(out=shift[:], in0=vt[:, 8 + 2 * n:8 + 3 * n], in1=gain[:])
-            nc.vector.tensor_sub(out=shift[:], in0=vt[:, 8 + n:8 + 2 * n], in1=shift[:])
-
-        def prep_clamp(pre, gain, shift, bias, mask, part, lo, hi):
-            nc.vector.tensor_mul(out=bias[:], in0=pre, in1=gain[:])
-            nc.vector.tensor_add(out=bias[:], in0=bias[:], in1=shift[:])
-            nc.vector.tensor_scalar(out=mask[:], in0=gain[:], scalar1=0.0, scalar2=None, op0=ALU.is_ge)
-            nc.vector.tensor_mul(out=part[:], in0=mask[:], in1=shift[:])
-            nc.vector.tensor_scalar(out=lo[:], in0=mask[:], scalar1=-1.0, scalar2=BIG, op0=ALU.add, op1=ALU.mult)
-            nc.vector.tensor_add(out=lo[:], in0=lo[:], in1=part[:])
-            nc.vector.tensor_sub(out=part[:], in0=shift[:], in1=part[:])
-            nc.vector.scalar_tensor_tensor(out=hi[:], in0=mask[:], scalar=BIG, in1=part[:], op0=ALU.mult, op1=ALU.add)
+            nc.gpsimd.tensor_tensor(out=gain[:], in0=vt[:, 8:8 + n], in1=gain[:], op=ALU.mult)
+            nc.gpsimd.tensor_tensor(out=shift[:], in0=vt[:, 8 + 2 * n:8 + 3 * n], in1=gain[:], op=ALU.mult)
+            nc.gpsimd.tensor_tensor(out=shift[:], in0=vt[:, 8 + n:8 + 2 * n], in1=shift[:], op=ALU.subtract)
+            if two_biases:
+                nc.gpsimd.tensor_tensor(out=bias[:], in0=vt[:, 0:n], in1=vt[:, n:2 * n], op=ALU.add)
+                nc.gpsimd.tensor_tensor(out=bias[:], in0=bias[:], in1=gain[:], op=ALU.mult)
+            else:
+                nc.gpsimd.tensor_tensor(out=bias[:], in0=vt[:, 0:n], in1=gain[:], op=ALU.mult)
+            nc.gpsimd.tensor_tensor(out=bias[:], in0=bias[:], in1=shift[:], op=ALU.add)
+            nc.gpsimd.tensor_scalar(out=mask[:], in0=gain[:], scalar1=0.0, scalar2=None, op0=ALU.is_ge)
+            nc.gpsimd.tensor_tensor(out=part[:], in0=mask[:], in1=shift[:], op=ALU.mult)
+            nc.gpsimd.tensor_scalar(out=lo[:], in0=mask[:], scalar1=-1.0, scalar2=BIG, op0=ALU.add, op1=ALU.mult)
+            nc.gpsimd.tensor_tensor(out=lo[:], in0=lo[:], in1=part[:], op=ALU.add)
+            nc.gpsimd.tensor_tensor(out=part[:], in0=shift[:], in1=part[:], op=ALU.subtract)
+            nc.gpsimd.tensor_scalar(out=hi[:], in0=mask[:], scalar1=BIG, scalar2=0.0, op0=ALU.mult, op1=ALU.add)
+            nc.gpsimd.tensor_tensor(out=hi[:], in0=hi[:], in1=part[:], op=ALU.add)
 
         def prep_bn1():
-            nc.vector.tensor_copy(out=vt1[:].rearrange("p (m e) -> p e m", e=2), in_=live["rows1"][:, :, 0:20])
-            prep_vectors(vt1, 8, gain1, shift1)
-            prep_clamp(vt1[:, 0:8], gain1, shift1, bias1, mask1, part1, lo1, hi1)
+            tp1 = ps_t.tile([P, 2, P], BF16, name="tp", tag="tp")
+            for e in range(2):
+                nc.tensor.transpose(tp1[:, e, :], rows1[:, e:2 * P:2], ident_b[:])
+            bn_constants(tp1[:, :, 0:20], vt1, vt1[:].rearrange("p (m e) -> p e m", e=2), 8, gain1, shift1, bias1, mask1, part1, lo1, hi1, False)
 
         def prep_bn2():
-            nc.vector.tensor_copy(out=vt2[:], in_=live["rows2"][:, 0:24])
-            prep_vectors(vt2, 4, gain2, shift2)
-            nc.vector.tensor_add(out=bsum[:], in0=vt2[:, 0:4], in1=vt2[:, 4:8])
-            prep_clamp(bsum[:], gain2, shift2, bias2, mask2, part2, lo2, hi2)
+            tp2 = ps_t.tile([P, P], BF16, name="tp", tag="tp")
+            nc.tensor.transpose(tp2[:], rows2[:], ident_b[:])
+            bn_constants(tp2[:, 0:24], vt2, vt2[:], 4, gain2, shift2, bias2, mask2, part2, lo2, hi2, True)
 
         def a_T(g, jj):
             tp = ps_t.tile([P, 1024], BF16, name="tp", tag="tp")
@@ -304,156 +291,101 @@ def tile_autoregressiveresidualblock_kernel(
             evac(eng, yt[:], live["oT", oi, h][:])
             nc.sync.dma_start(out=out_r[:, 4 * h:4 * h + 4, P * oi:P * oi + P], in_=yt[:])
 
-        gj = ((0, 0), (1, 0), (0, 1), (1, 1))
-
         def T(u):
             if u[0] == "a":
                 a_T(u[1], u[2])
-            elif u[0] == "w":
-                w_T(u[1], u[2], u[3])
             else:
-                q_T(u[1], u[2])
+                w_T(u[0], u[1], u[2])
 
         def C(u, eng):
             if u[0] == "a":
                 a_C(u[1], u[2], eng)
-            elif u[0] == "w":
-                w_C(u[1], u[2], u[3], eng)
             else:
-                q_C(u[1], u[2], eng)
+                w_C(u[0], u[1], u[2], eng)
 
         def Q(u):
             if u[0] == "a":
                 a_Q(u[1], u[2])
-            elif u[0] == "w":
-                w_Q(u[1], u[2], u[3])
+            else:
+                w_Q(u[0], u[1], u[2])
 
-        def t_run(units, engs):
-            for u, e in zip(units, engs):
+        def operand_run(units, engs, lag):
+            for k, u in enumerate(units):
                 T(u)
-                C(u, e)
-
-        def q_run(units):
-            for u in units:
+                C(u, engs[k % len(engs)])
+                if k >= lag:
+                    Q(units[k - lag])
+            for u in units[len(units) - lag:]:
                 Q(u)
 
-        def l1_run(ms, h):
-            for i in ms:
-                l1_M(i, h)
-                l1_E(i, h)
-
-        def clamps(ms, h):
-            for i in ms:
-                l1_A(i, h)
-
-        def ua(h):
-            return [("a", g, 2 * h + j) for j, g in gj]
-
-        def uw(nm, lst):
-            return [("w", nm, g, j) for g, j in lst]
-
-        def uq(h):
-            return [("q", G, h) for G in range(4)]
-
-        AD = ("act", "dve", "act", "dve")
-        AA = ("act", "act", "act", "act")
-
-        def l2o_fin(oi, h):
-            l2o_E(oi, h)
-            l2o_A(oi, h)
+        def queue_run(h, Gs):
+            for G in Gs:
+                q_T(G, h)
+                q_C(G, h, "act")
 
         load_a(0)
+        load_w1((0,))
         load_a(1)
-        load_w1()
+        load_w1((1, 2, 3))
         load_a(2)
         load_q2(0)
         load_ws()
         load_w2()
-        load_q2(1)
         load_rows2()
+        load_q2(1)
 
-        def w4(nm, lst):
-            return uw(nm, lst)
+        ctx.enter_context(tc.manual_schedule(engines={mybir.EngineType.PE}))
 
-        A0 = ua(0)
-        A1 = ua(1)
-        W1a = w4("w1", ((0, 0), (1, 0), (0, 1), (1, 1)))
-        W1b = w4("w1", ((0, 2), (1, 2), (0, 3), (1, 3)))
-        WS = w4("ws", ((0, 0), (0, 1), (1, 0), (1, 1)))
-        W2a = w4("w2", ((0, 0), (0, 1), (1, 0), (1, 1)))
-        W2b = w4("w2", ((2, 0), (2, 1), (3, 0), (3, 1)))
-        Q0 = uq(0)
-        Q1 = uq(1)
+        a_units = [("a", g, j) for j in range(4) for g in range(2)]
+        w1_units = [("w1", g, j) for j in range(4) for g in range(2)]
+        ws_units = [("ws", g, j) for j in range(2) for g in range(2)]
+        w2_units = [("w2", g, j) for j in range(2) for g in range(4)]
 
-        t_run(A0[0:2], AD)
-        t_run(A0[2:4], AD)
-        q_run(A0)
-        t_run(W1a, AD)
-        prep_T1()
-        q_run(W1a)
+        operand_run(a_units[0:2] + w1_units[0:2] + a_units[2:4], ("dve", "act"), 2)
         prep_bn1()
-        l1_run((0, 1), 0)
-        t_run(W1b, AD)
-        q_run(W1b)
-        clamps((0, 1), 0)
-        l1_run((2, 3), 0)
-        t_run(A1[0:2], AD)
-        q_run(A1[0:2])
-        clamps((2, 3), 0)
-        l1_run((4, 5), 0)
-        t_run(A1[2:4], AD)
-        q_run(A1[2:4])
-        clamps((4, 5), 0)
-        l1_run((6, 7), 0)
-        t_run(Q0[0:2], AA)
-        clamps((6, 7), 0)
-        g_R(0, 0)
-        l1_run((0, 1), 1)
-        t_run(Q0[2:4], AA)
-        g_R(1, 0)
-        g_Q(0, 0)
-        clamps((0, 1), 1)
-        g_Q(1, 0)
-        l1_run((2, 3), 1)
-        t_run(WS, CW)
-        g_R(2, 0)
-        q_run(WS)
-        clamps((2, 3), 1)
-        g_R(3, 0)
-        g_Q(2, 0)
-        l1_run((4, 5), 1)
-        t_run(W2a, CW)
-        g_Q(3, 0)
-        q_run(W2a)
-        clamps((4, 5), 1)
-        l1_run((6, 7), 1)
-        t_run(W2b, CW)
-        q_run(W2b)
-        clamps((6, 7), 1)
-        l2o_M(0, 0, (0, 1))
-        l2o_M(1, 0, (0, 1))
-        t_run(Q1[0:2], AA)
-        prep_T2()
+        operand_run(w1_units[2:], ("dve", "act"), 2)
+        for i in range(8):
+            l1_M(i, 0)
+            l1_E(i, 0)
+            l1_A(i, 0)
+        operand_run(a_units[4:8], ("act",), 2)
+        queue_run(0, range(4))
+        operand_run(ws_units, ("act", "dve"), 2)
+        for i in range(8):
+            l1_M(i, 1)
+            l1_E(i, 1)
+        for G in range(4):
+            g_R(G, 0)
+        for G in range(4):
+            g_Q(G, 0)
+        operand_run(w2_units[0:4], ("act",), 2)
+        queue_run(1, (0, 1))
+        operand_run(w2_units[4:8], ("act",), 2)
         prep_bn2()
-        g_R(0, 1)
-        l2o_M(2, 0, (0, 1))
-        l2o_M(3, 0, (0, 1))
-        t_run(Q1[2:4], AA)
-        groups = [(oi, 0) for oi in range(4)] + [(oi, 1) for oi in range(4)]
+        queue_run(1, (2, 3))
+        for i in range(8):
+            l1_A(i, 1)
+        g_R(2, 1, "act")
+        for G in (0, 1, 3):
+            g_R(G, 1)
+        for G in (0, 1, 2, 3):
+            g_Q(G, 1)
 
-        def out_T(ks):
-            for k in ks:
-                l2o_T(groups[k][0], groups[k][1])
-                l2o_S(groups[k][0], groups[k][1], ("act", "dve")[k % 2])
+        def out_run(ois, h):
+            for oi in ois:
+                l2o_T(oi, h)
+                l2o_S(oi, h, ("dve", "act")[oi % 2])
 
-        for n, (oi, h) in enumerate(groups):
-            l2o_M(oi, h, (2, 3, 4, 5) if h == 0 else (0, 1, 2, 3, 4, 5))
-            l2o_E(oi, h)
-            if h == 0:
-                if oi < 3:
-                    g_R(oi + 1, 1)
-                g_Q(oi, 1)
-            l2o_A(oi, h)
-            if n % 2 == 1 and n >= 3:
-                out_T((n - 3, n - 2))
-        out_T((6, 7))
+        for oi in range(4):
+            l2o_M(oi, 0, (0, 1, 2, 3, 4, 5))
+            l2o_E(oi, 0)
+            l2o_A(oi, 0)
+        for oi in range(4):
+            l2o_M(oi, 1, (0, 1, 2, 3, 4, 5))
+            l2o_E(oi, 1)
+            l2o_A(oi, 1)
+            if oi == 1:
+                out_run((0, 1), 0)
+            if oi == 2:
+                out_run((2, 3), 0)
+        out_run((0, 1, 2, 3), 1)

@@ -46,6 +46,8 @@ def tile_autoregressiveresidualblock_kernel(
 
         rows1 = const.tile([P, 2 * P], BF16, name="rows1", tag="rows1")
         rows2 = const.tile([P, P], BF16, name="rows2", tag="rows2")
+        zeros = const.tile([P, 512], BF16, name="zeros", tag="zeros")
+        nc.vector.memset(zeros[:], 0.0)
         nc.vector.memset(rows1[:], 0.0)
         nc.vector.memset(rows2[:], 0.0)
         for n, vec in enumerate((b1, bn1_scale, bn1_bias, bn1_mean, bn1_var)):
@@ -256,6 +258,7 @@ def tile_autoregressiveresidualblock_kernel(
             acc = live["l2o", oi, h]
             rows = slice(P * oi, P * oi + P)
             cols = slice(512 * h, 512 * h + 512)
+            last = 5 if h == 0 else 4
             for part in parts:
                 if part < 2:
                     lc, ls, rc, rs, g = ws_c, ws_s, a_c, a_s, part
@@ -265,7 +268,7 @@ def tile_autoregressiveresidualblock_kernel(
                     out=acc[:],
                     lhsT=lc[:, g, rows].bitcast(FP8X4), lhsT_scale=ls[:, g, rows],
                     rhs=rc[:, g, cols].bitcast(FP8X4), rhs_scale=rs[:, g, cols],
-                    start=(part == 0), stop=(part == 5),
+                    start=(part == 0), stop=(part == last),
                 )
 
         def l2o_E(oi, h):
@@ -328,8 +331,8 @@ def tile_autoregressiveresidualblock_kernel(
         load_a(1)
         load_w1((1, 2, 3))
         load_a(2)
-        load_q2(0)
         load_ws()
+        load_q2(0)
         load_w2()
         load_rows2()
         load_q2(1)
@@ -341,34 +344,42 @@ def tile_autoregressiveresidualblock_kernel(
         ws_units = [("ws", g, j) for j in range(2) for g in range(2)]
         w2_units = [("w2", g, j) for j in range(2) for g in range(4)]
 
-        operand_run(a_units[0:2] + w1_units[0:2] + a_units[2:4], ("dve", "act"), 2)
+        def l1_run(ms, h):
+            for i in ms:
+                l1_M(i, h)
+                l1_E(i, h)
+                if h == 0:
+                    l1_A(i, h)
+
+        idle = ps_t.tile([P, 512], F32, name="tp", tag="tp")
+        for n in range(5):
+            nc.tensor.matmul(idle[:], lhsT=zeros[:, 0:P], rhs=zeros[:], start=True, stop=True)
+        operand_run(a_units[0:2] + w1_units[0:2] + a_units[2:4] + w1_units[2:4], ("act", "act", "dve"), 2)
         prep_bn1()
-        operand_run(w1_units[2:], ("dve", "act"), 2)
-        for i in range(8):
-            l1_M(i, 0)
-            l1_E(i, 0)
-            l1_A(i, 0)
+        operand_run(w1_units[4:8], ("act", "act", "dve"), 2)
+        l1_run(range(0, 4), 0)
         operand_run(a_units[4:8], ("act",), 2)
-        queue_run(0, range(4))
+        l1_run(range(4, 8), 0)
         operand_run(ws_units, ("act", "dve"), 2)
-        for i in range(8):
-            l1_M(i, 1)
-            l1_E(i, 1)
+        l1_run(range(0, 4), 1)
+        queue_run(0, range(4))
+        l1_run(range(4, 8), 1)
+        operand_run(w2_units[0:4], ("act",), 2)
+        prep_bn2()
         for G in range(4):
             g_R(G, 0)
         for G in range(4):
             g_Q(G, 0)
-        operand_run(w2_units[0:4], ("act",), 2)
-        queue_run(1, (0, 1))
+        for oi in range(4):
+            l2o_M(oi, 0, (0, 1))
+        queue_run(1, range(4))
         operand_run(w2_units[4:8], ("act",), 2)
-        prep_bn2()
-        queue_run(1, (2, 3))
         for i in range(8):
             l1_A(i, 1)
         g_R(2, 1, "act")
         for G in (0, 1, 3):
             g_R(G, 1)
-        for G in (0, 1, 2, 3):
+        for G in (0, 1, 3, 2):
             g_Q(G, 1)
 
         def out_run(ois, h):
@@ -377,11 +388,11 @@ def tile_autoregressiveresidualblock_kernel(
                 l2o_S(oi, h, ("dve", "act")[oi % 2])
 
         for oi in range(4):
-            l2o_M(oi, 0, (0, 1, 2, 3, 4, 5))
+            l2o_M(oi, 0, (2, 3, 4, 5))
             l2o_E(oi, 0)
             l2o_A(oi, 0)
         for oi in range(4):
-            l2o_M(oi, 1, (0, 1, 2, 3, 4, 5))
+            l2o_M(oi, 1, (0, 1, 2, 3, 5, 4))
             l2o_E(oi, 1)
             l2o_A(oi, 1)
             if oi == 1:

@@ -64,7 +64,7 @@ def tile_autoregressiveresidualblock_kernel(
         a_chunks = ((0, 2), (2, 2), (4, 4))
         a_sb = [raw.tile([P, 2, nt, DIN], BF16, name=f"a_sb{t0}", tag=f"a_sb{t0}") for t0, nt in a_chunks]
         q2_sb = raw.tile([P, 8 * MID], BF16, name="q2_sb", tag="q2_sb")
-        w1_sb = raw.tile([P, 8 * 2 * DIN], BF16, name="w1_sb", tag="w1_sb")
+        w1_sb = [raw.tile([P, 4 * DIN], BF16, name=f"w1_sb{j}", tag=f"w1_sb{j}") for j in range(4)]
         ws_sb = raw.tile([P, 4 * 2 * DIN], BF16, name="ws_sb", tag="ws_sb")
         w2_sb = raw.tile([P, 4 * 2 * MID], BF16, name="w2_sb", tag="w2_sb")
         a_of = {t0 + k: (tile, k) for (t0, nt), tile in zip(a_chunks, a_sb) for k in range(nt)}
@@ -87,7 +87,7 @@ def tile_autoregressiveresidualblock_kernel(
 
         def load_w1(prs):
             for pr in prs:
-                nc.sync.dma_start(out=w1_sb[:, 4 * DIN * pr:4 * DIN * pr + 4 * DIN], in_=w1_v[:, pr, :])
+                nc.sync.dma_start(out=w1_sb[pr][:], in_=w1_v[:, pr, :])
 
         def load_q2(h):
             nc.sync.dma_start(out=q2_t[:, 4 * h:4 * h + 4, :], in_=q2_v[:, 4 * h:4 * h + 4, :])
@@ -96,8 +96,8 @@ def tile_autoregressiveresidualblock_kernel(
             nc.sync.dma_start(out=ws_t, in_=ws_v)
 
         def load_rows2():
-            for n, vec in enumerate((b2, b_skip, bn2_scale, bn2_bias, bn2_mean, bn2_var)):
-                nc.sync.dma_start(out=rows2[4 * n:4 * n + 4, :], in_=vec.rearrange("(i p) -> i p", p=P))
+            for n, vec in enumerate((b2, bn2_scale, bn2_bias, bn2_mean, bn2_var, b_skip)):
+                nc.scalar.dma_start(out=rows2[4 * n:4 * n + 4, :], in_=vec.rearrange("(i p) -> i p", p=P))
 
         def load_w2():
             for pr in range(2):
@@ -114,60 +114,45 @@ def tile_autoregressiveresidualblock_kernel(
         w2_c = keep.tile([P, 4, OUT], U32, name="w2_c", tag="w2_c", align_bytes=64)
         w2_s = keep.tile([P, 4, OUT], U8, name="w2_s", tag="w2_s", align_bytes=64)
         weights = {
-            "w1": (w1_sb[:].bitcast(F32), DIN, w1_c, w1_s),
-            "ws": (ws_sb[:].bitcast(F32), DIN, ws_c, ws_s),
-            "w2": (w2_sb[:].bitcast(F32), MID, w2_c, w2_s),
+            "w1": (w1_c, w1_s),
+            "ws": (ws_c, ws_s),
+            "w2": (w2_c, w2_s),
         }
 
-        vt1 = const.tile([P, 40], F32, name="vt1", tag="vt1")
-        gain1 = const.tile([P, 8], F32, name="gain1", tag="gain1")
-        shift1 = const.tile([P, 8], F32, name="shift1", tag="shift1")
-        bias1 = const.tile([P, 8], F32, name="bias1", tag="bias1")
-        mask1 = const.tile([P, 8], F32, name="mask1", tag="mask1")
-        part1 = const.tile([P, 8], F32, name="part1", tag="part1")
-        lo1 = const.tile([P, 8], F32, name="lo1", tag="lo1")
-        hi1 = const.tile([P, 8], F32, name="hi1", tag="hi1")
-        vt2 = const.tile([P, 24], F32, name="vt2", tag="vt2")
-        gain2 = const.tile([P, 4], F32, name="gain2", tag="gain2")
-        shift2 = const.tile([P, 4], F32, name="shift2", tag="shift2")
-        bias2 = const.tile([P, 4], F32, name="bias2", tag="bias2")
-        mask2 = const.tile([P, 4], F32, name="mask2", tag="mask2")
-        part2 = const.tile([P, 4], F32, name="part2", tag="part2")
-        lo2 = const.tile([P, 4], F32, name="lo2", tag="lo2")
-        hi2 = const.tile([P, 4], F32, name="hi2", tag="hi2")
+        vt = const.tile([P, 5, 12], F32, name="vt", tag="vt")
+        skip = const.tile([P, 4], F32, name="skip", tag="skip")
+        gain = const.tile([P, 12], F32, name="gain", tag="gain")
+        shift = const.tile([P, 12], F32, name="shift", tag="shift")
+        bias = const.tile([P, 12], F32, name="bias", tag="bias")
+        pos = const.tile([P, 12], F32, name="pos", tag="pos")
+        neg = const.tile([P, 12], F32, name="neg", tag="neg")
+        lo = const.tile([P, 12], F32, name="lo", tag="lo")
+        hi = const.tile([P, 12], F32, name="hi", tag="hi")
 
-        def bn_constants(tp_view, vt, vt_view, n, gain, shift, bias, mask, part, lo, hi, two_biases):
-            nc.vector.tensor_copy(out=vt_view, in_=tp_view)
-            nc.gpsimd.tensor_scalar(out=gain[:], in0=vt[:, 8 + 3 * n:8 + 4 * n], scalar1=1.0, scalar2=EPS, op0=ALU.mult, op1=ALU.add)
+        def prep_bn():
+            tp = ps_t.tile([P, 3, P], BF16, name="tp", tag="tp")
+            for e in range(2):
+                nc.tensor.transpose(tp[:, e, :], rows1[:, e:2 * P:2], ident_b[:])
+            nc.tensor.transpose(tp[:, 2, :], rows2[:], ident_b[:])
+            nc.vector.tensor_copy(
+                out=vt[:, :, 0:8].rearrange("p n (g e) -> p e n g", e=2),
+                in_=tp[:, 0:2, 0:20].rearrange("p e (n g) -> p e n g", g=4),
+            )
+            nc.vector.tensor_copy(out=vt[:, :, 8:12], in_=tp[:, 2, 0:20].rearrange("p (n i) -> p n i", i=4))
+            nc.vector.tensor_copy(out=skip[:], in_=tp[:, 2, 20:24])
+            nc.vector.tensor_add(out=vt[:, 0, 8:12], in0=vt[:, 0, 8:12], in1=skip[:])
+            nc.vector.tensor_scalar_add(out=gain[:], in0=vt[:, 4, :], scalar1=EPS)
             nc.scalar.activation(out=gain[:], in_=gain[:], func=ACTF.Sqrt)
             nc.vector.reciprocal(out=gain[:], in_=gain[:])
-            nc.gpsimd.tensor_tensor(out=gain[:], in0=vt[:, 8:8 + n], in1=gain[:], op=ALU.mult)
-            nc.gpsimd.tensor_tensor(out=shift[:], in0=vt[:, 8 + 2 * n:8 + 3 * n], in1=gain[:], op=ALU.mult)
-            nc.gpsimd.tensor_tensor(out=shift[:], in0=vt[:, 8 + n:8 + 2 * n], in1=shift[:], op=ALU.subtract)
-            if two_biases:
-                nc.gpsimd.tensor_tensor(out=bias[:], in0=vt[:, 0:n], in1=vt[:, n:2 * n], op=ALU.add)
-                nc.gpsimd.tensor_tensor(out=bias[:], in0=bias[:], in1=gain[:], op=ALU.mult)
-            else:
-                nc.gpsimd.tensor_tensor(out=bias[:], in0=vt[:, 0:n], in1=gain[:], op=ALU.mult)
-            nc.gpsimd.tensor_tensor(out=bias[:], in0=bias[:], in1=shift[:], op=ALU.add)
-            nc.gpsimd.tensor_scalar(out=mask[:], in0=gain[:], scalar1=0.0, scalar2=None, op0=ALU.is_ge)
-            nc.gpsimd.tensor_tensor(out=part[:], in0=mask[:], in1=shift[:], op=ALU.mult)
-            nc.gpsimd.tensor_scalar(out=lo[:], in0=mask[:], scalar1=-1.0, scalar2=BIG, op0=ALU.add, op1=ALU.mult)
-            nc.gpsimd.tensor_tensor(out=lo[:], in0=lo[:], in1=part[:], op=ALU.add)
-            nc.gpsimd.tensor_tensor(out=part[:], in0=shift[:], in1=part[:], op=ALU.subtract)
-            nc.gpsimd.tensor_scalar(out=hi[:], in0=mask[:], scalar1=BIG, scalar2=0.0, op0=ALU.mult, op1=ALU.add)
-            nc.gpsimd.tensor_tensor(out=hi[:], in0=hi[:], in1=part[:], op=ALU.add)
-
-        def prep_bn1():
-            tp1 = ps_t.tile([P, 2, P], BF16, name="tp", tag="tp")
-            for e in range(2):
-                nc.tensor.transpose(tp1[:, e, :], rows1[:, e:2 * P:2], ident_b[:])
-            bn_constants(tp1[:, :, 0:20], vt1, vt1[:].rearrange("p (m e) -> p e m", e=2), 8, gain1, shift1, bias1, mask1, part1, lo1, hi1, False)
-
-        def prep_bn2():
-            tp2 = ps_t.tile([P, P], BF16, name="tp", tag="tp")
-            nc.tensor.transpose(tp2[:], rows2[:], ident_b[:])
-            bn_constants(tp2[:, 0:24], vt2, vt2[:], 4, gain2, shift2, bias2, mask2, part2, lo2, hi2, True)
+            nc.vector.tensor_mul(out=gain[:], in0=vt[:, 1, :], in1=gain[:])
+            nc.vector.tensor_mul(out=shift[:], in0=vt[:, 3, :], in1=gain[:])
+            nc.vector.tensor_sub(out=shift[:], in0=vt[:, 2, :], in1=shift[:])
+            nc.vector.tensor_mul(out=bias[:], in0=vt[:, 0, :], in1=gain[:])
+            nc.vector.tensor_add(out=bias[:], in0=bias[:], in1=shift[:])
+            nc.vector.tensor_scalar(out=pos[:], in0=gain[:], scalar1=0.0, scalar2=None, op0=ALU.is_ge)
+            nc.vector.tensor_scalar(out=neg[:], in0=pos[:], scalar1=-1.0, scalar2=None, op0=ALU.add)
+            nc.vector.scalar_tensor_tensor(out=lo[:], in0=neg[:], scalar=BIG, in1=shift[:], op0=ALU.mult, op1=ALU.add)
+            nc.vector.scalar_tensor_tensor(out=hi[:], in0=pos[:], scalar=BIG, in1=shift[:], op0=ALU.mult, op1=ALU.add)
 
         def a_T(g, jj):
             tp = ps_t.tile([P, 1024], BF16, name="tp", tag="tp")
@@ -188,13 +173,32 @@ def tile_autoregressiveresidualblock_kernel(
             cols = slice(256 * jj, 256 * jj + 256)
             nc.vector.quantize_mx(out=a_c[:, g, cols].bitcast(FP8X4), scales=a_s[:, g, cols], in_=live["aC", g, jj][:])
 
+        sorted_tags = {"ws": ("a_sb0", "a_sb2"), "w2": ("w1_sb0", "w1_sb1", "w1_sb2", "w1_sb3")}
+
+        def w_W(nm, n):
+            src = {"ws": ws_sb, "w2": w2_sb}[nm]
+            dst = raw.tile([P, 1024], F32, name="wsort", tag=sorted_tags[nm][n])
+            nc.vector.tensor_copy(
+                out=dst[:].rearrange("p (x u q) -> p x u q", u=2, q=P),
+                in_=src[:].bitcast(F32)[:, 1024 * n:1024 * n + 1024].rearrange("p (x q u) -> p x u q", u=2, q=P),
+            )
+            live["wW", nm, n] = dst
+
+        def w_src(nm, g, j, ii, u):
+            if nm == "w1":
+                c0 = 512 * ii + 256 * g
+                return w1_sb[j][:].bitcast(F32)[:, c0 + u:c0 + 256:2]
+            if nm == "ws":
+                c0 = P * ((2 * ii + g) * 2 + u)
+                return live["wW", "ws", j][:, c0:c0 + P]
+            c0 = P * (2 * g + u)
+            return live["wW", "w2", 2 * j + ii][:, c0:c0 + P]
+
         def w_T(nm, g, j):
-            wf, kw = weights[nm][0], weights[nm][1]
             tp = ps_t.tile([P, 2, 256], F32, name="tp", tag="tp")
             for ii in range(2):
                 for u in range(2):
-                    c0 = (2 * j + ii) * kw + 256 * g
-                    nc.tensor.transpose(tp[:, u, P * ii:P * ii + P], wf[:, c0 + u:c0 + 256:2], ident_f[:])
+                    nc.tensor.transpose(tp[:, u, P * ii:P * ii + P], w_src(nm, g, j, ii, u), ident_f[:])
             live["wT", nm, g, j] = tp
 
         def w_C(nm, g, j, eng):
@@ -204,7 +208,7 @@ def tile_autoregressiveresidualblock_kernel(
 
         def w_Q(nm, g, j):
             cols = slice(256 * j, 256 * j + 256)
-            nc.vector.quantize_mx(out=weights[nm][2][:, g, cols].bitcast(FP8X4), scales=weights[nm][3][:, g, cols], in_=live["wC", nm, g, j][:])
+            nc.vector.quantize_mx(out=weights[nm][0][:, g, cols].bitcast(FP8X4), scales=weights[nm][1][:, g, cols], in_=live["wC", nm, g, j][:])
 
         def s_tile(G, h):
             if ("S", G, h) not in live:
@@ -234,13 +238,13 @@ def tile_autoregressiveresidualblock_kernel(
 
         def l1_E(i, h):
             v = v_pool.tile([P, 512], BF16, name="vlin", tag="vlin")
-            nc.scalar.activation(out=v[:], in_=live["l1", i, h][:], func=ACTF.Identity, bias=bias1[:, i:i + 1], scale=gain1[:, i:i + 1])
+            nc.scalar.activation(out=v[:], in_=live["l1", i, h][:], func=ACTF.Identity, bias=bias[:, i:i + 1], scale=gain[:, i:i + 1])
             live["v", i, h] = v
 
         def l1_A(i, h):
             nc.vector.tensor_scalar(
                 out=s_tile(i // 2, h)[:, 2 * (i % 2) + 1, :], in0=live["v", i, h][:],
-                scalar1=lo1[:, i:i + 1], scalar2=hi1[:, i:i + 1], op0=ALU.max, op1=ALU.min,
+                scalar1=lo[:, i:i + 1], scalar2=hi[:, i:i + 1], op0=ALU.max, op1=ALU.min,
             )
 
         def g_R(G, h, eng="dve"):
@@ -273,12 +277,12 @@ def tile_autoregressiveresidualblock_kernel(
 
         def l2o_E(oi, h):
             v = o_pool.tile([P, 512], F32, name="olin", tag="olin")
-            nc.scalar.activation(out=v[:], in_=live["l2o", oi, h][:], func=ACTF.Identity, bias=bias2[:, oi:oi + 1], scale=gain2[:, oi:oi + 1])
+            nc.scalar.activation(out=v[:], in_=live["l2o", oi, h][:], func=ACTF.Identity, bias=bias[:, 8 + oi:9 + oi], scale=gain[:, 8 + oi:9 + oi])
             live["ov", oi, h] = v
 
         def l2o_A(oi, h):
             y = o_pool.tile([P, 512], F32, name="ocl", tag="ocl", align_bytes=64)
-            nc.vector.tensor_scalar(out=y[:], in0=live["ov", oi, h][:], scalar1=lo2[:, oi:oi + 1], scalar2=hi2[:, oi:oi + 1], op0=ALU.max, op1=ALU.min)
+            nc.vector.tensor_scalar(out=y[:], in0=live["ov", oi, h][:], scalar1=lo[:, 8 + oi:9 + oi], scalar2=hi[:, 8 + oi:9 + oi], op0=ALU.max, op1=ALU.min)
             live["oy", oi, h] = y
 
         out_r = out.rearrange("(m t) c o -> m t (c o)", t=8)
@@ -321,10 +325,10 @@ def tile_autoregressiveresidualblock_kernel(
             for u in units[len(units) - lag:]:
                 Q(u)
 
-        def queue_run(h, Gs):
-            for G in Gs:
+        def queue_run(h, engs):
+            for G in range(4):
                 q_T(G, h)
-                q_C(G, h, "act")
+                q_C(G, h, engs[G % len(engs)])
 
         load_a(0)
         load_w1((0,))
@@ -334,7 +338,6 @@ def tile_autoregressiveresidualblock_kernel(
         load_ws()
         load_q2(0)
         load_w2()
-        load_rows2()
         load_q2(1)
 
         ctx.enter_context(tc.manual_schedule(engines={mybir.EngineType.PE}))
@@ -352,28 +355,33 @@ def tile_autoregressiveresidualblock_kernel(
                     l1_A(i, h)
 
         idle = ps_t.tile([P, 512], F32, name="tp", tag="tp")
-        for n in range(5):
+        for n in range(4):
             nc.tensor.matmul(idle[:], lhsT=zeros[:, 0:P], rhs=zeros[:], start=True, stop=True)
-        operand_run(a_units[0:2] + w1_units[0:2] + a_units[2:4] + w1_units[2:4], ("act", "act", "dve"), 2)
-        prep_bn1()
-        operand_run(w1_units[4:8], ("act", "act", "dve"), 2)
+        operand_run(a_units[0:2] + w1_units[0:2] + a_units[2:4] + w1_units[2:4], ("dve", "act", "act"), 2)
+        load_rows2()
+        prep_bn()
+        operand_run(w1_units[4:8], ("dve", "act", "act"), 2)
         l1_run(range(0, 4), 0)
         operand_run(a_units[4:8], ("act",), 2)
+        for n in range(2):
+            w_W("ws", n)
+        operand_run(ws_units, ("act", "act", "dve"), 2)
         l1_run(range(4, 8), 0)
-        operand_run(ws_units, ("act", "dve"), 2)
-        l1_run(range(0, 4), 1)
-        queue_run(0, range(4))
-        l1_run(range(4, 8), 1)
+        queue_run(0, ("act",))
+        l1_run(range(0, 8), 1)
+        for n in range(2):
+            w_W("w2", n)
         operand_run(w2_units[0:4], ("act",), 2)
-        prep_bn2()
+        for oi in range(4):
+            l2o_M(oi, 0, (0, 1))
+        for n in range(2, 4):
+            w_W("w2", n)
+        operand_run(w2_units[4:8], ("act",), 2)
         for G in range(4):
             g_R(G, 0)
         for G in range(4):
             g_Q(G, 0)
-        for oi in range(4):
-            l2o_M(oi, 0, (0, 1))
-        queue_run(1, range(4))
-        operand_run(w2_units[4:8], ("act",), 2)
+        queue_run(1, ("act", "act", "dve"))
         for i in range(8):
             l1_A(i, 1)
         g_R(2, 1, "act")
@@ -392,7 +400,9 @@ def tile_autoregressiveresidualblock_kernel(
             l2o_E(oi, 0)
             l2o_A(oi, 0)
         for oi in range(4):
-            l2o_M(oi, 1, (0, 1, 2, 3, 5, 4))
+            l2o_M(oi, 1, (0, 1))
+        for oi in range(4):
+            l2o_M(oi, 1, (2, 3, 5, 4))
             l2o_E(oi, 1)
             l2o_A(oi, 1)
             if oi == 1:

@@ -256,13 +256,14 @@ def tile_autoregressiveresidualblock_kernel(
             cols = slice(512 * h, 512 * h + 512)
             nc.vector.quantize_mx(out=g_c[:, G, cols].bitcast(FP8X4), scales=g_s[:, G, cols], in_=live["gg", G, h][:])
 
-        def l2o_M(oi, h, parts):
-            if ("l2o", oi, h) not in live:
-                live["l2o", oi, h] = ps_a.tile([P, 512], F32, name="acc", tag="acc")
-            acc = live["l2o", oi, h]
+        out_r = out.rearrange("(m t) c o -> m t (c o)", t=8)
+
+        def l2_M(oi, c0, w, parts, stop):
+            if ("l2", oi, c0) not in live:
+                live["l2", oi, c0] = ps_a.tile([P, w], F32, name="acc", tag="acc")
+            acc = live["l2", oi, c0]
             rows = slice(P * oi, P * oi + P)
-            cols = slice(512 * h, 512 * h + 512)
-            last = 5 if h == 0 else 4
+            cols = slice(c0, c0 + w)
             for part in parts:
                 if part < 2:
                     lc, ls, rc, rs, g = ws_c, ws_s, a_c, a_s, part
@@ -272,31 +273,24 @@ def tile_autoregressiveresidualblock_kernel(
                     out=acc[:],
                     lhsT=lc[:, g, rows].bitcast(FP8X4), lhsT_scale=ls[:, g, rows],
                     rhs=rc[:, g, cols].bitcast(FP8X4), rhs_scale=rs[:, g, cols],
-                    start=(part == 0), stop=(part == last),
+                    start=(part == 0), stop=(part == stop),
                 )
 
-        def l2o_E(oi, h):
-            v = o_pool.tile([P, 512], F32, name="olin", tag="olin")
-            nc.scalar.activation(out=v[:], in_=live["l2o", oi, h][:], func=ACTF.Identity, bias=bias[:, 8 + oi:9 + oi], scale=gain[:, 8 + oi:9 + oi])
-            live["ov", oi, h] = v
+        def l2_E(oi, c0, w):
+            v = o_pool.tile([P, w], F32, name="olin", tag="olin")
+            nc.scalar.activation(out=v[:], in_=live["l2", oi, c0][:], func=ACTF.Identity, bias=bias[:, 8 + oi:9 + oi], scale=gain[:, 8 + oi:9 + oi])
+            y = o_pool.tile([P, w], F32, name="ocl", tag="ocl", align_bytes=64)
+            nc.vector.tensor_scalar(out=y[:], in0=v[:], scalar1=lo[:, 8 + oi:9 + oi], scalar2=hi[:, 8 + oi:9 + oi], op0=ALU.max, op1=ALU.min)
+            live["oy", oi, c0] = y
 
-        def l2o_A(oi, h):
-            y = o_pool.tile([P, 512], F32, name="ocl", tag="ocl", align_bytes=64)
-            nc.vector.tensor_scalar(out=y[:], in0=live["ov", oi, h][:], scalar1=lo[:, 8 + oi:9 + oi], scalar2=hi[:, 8 + oi:9 + oi], op0=ALU.max, op1=ALU.min)
-            live["oy", oi, h] = y
-
-        out_r = out.rearrange("(m t) c o -> m t (c o)", t=8)
-
-        def l2o_T(oi, h):
-            tp = ps_t.tile([P, 4, P], F32, name="tp", tag="tp")
-            for tt in range(4):
-                nc.tensor.transpose(tp[:, tt, :], live["oy", oi, h][:, P * tt:P * tt + P], ident_f[:])
-            live["oT", oi, h] = tp
-
-        def l2o_S(oi, h, eng):
-            yt = o_pool.tile([P, 4, P], F32, name="otr", tag="otr")
-            evac(eng, yt[:], live["oT", oi, h][:])
-            nc.sync.dma_start(out=out_r[:, 4 * h:4 * h + 4, P * oi:P * oi + P], in_=yt[:])
+        def l2_T(oi, c0, w, eng):
+            t0, nt = c0 // P, w // P
+            tp = ps_t.tile([P, nt, P], F32, name="tp", tag="tp")
+            for tt in range(nt):
+                nc.tensor.transpose(tp[:, tt, :], live["oy", oi, c0][:, P * tt:P * tt + P], ident_f[:])
+            yt = o_pool.tile([P, nt, P], F32, name="otr", tag="otr", bufs=6)
+            evac(eng, yt[:], tp[:])
+            nc.sync.dma_start(out=out_r[:, t0:t0 + nt, P * oi:P * oi + P], in_=yt[:])
 
         def T(u):
             if u[0] == "a":
@@ -354,10 +348,15 @@ def tile_autoregressiveresidualblock_kernel(
                 if h == 0:
                     l1_A(i, h)
 
-        idle = ps_t.tile([P, 512], F32, name="tp", tag="tp")
-        for n in range(4):
-            nc.tensor.matmul(idle[:], lhsT=zeros[:, 0:P], rhs=zeros[:], start=True, stop=True)
-        operand_run(a_units[0:2] + w1_units[0:2] + a_units[2:4] + w1_units[2:4], ("dve", "act", "act"), 2)
+        def idle_run(n):
+            idle = ps_t.tile([P, 512], F32, name="tp", tag="tp")
+            for k in range(n):
+                nc.tensor.matmul(idle[:], lhsT=zeros[:, 0:P], rhs=zeros[:], start=True, stop=True)
+
+        idle_run(5)
+        operand_run(a_units[0:2] + w1_units[0:2], ("dve", "act", "act"), 2)
+        idle_run(2)
+        operand_run(a_units[2:4] + w1_units[2:4], ("act", "act", "dve"), 2)
         load_rows2()
         prep_bn()
         operand_run(w1_units[4:8], ("dve", "act", "act"), 2)
@@ -373,7 +372,7 @@ def tile_autoregressiveresidualblock_kernel(
             w_W("w2", n)
         operand_run(w2_units[0:4], ("act",), 2)
         for oi in range(4):
-            l2o_M(oi, 0, (0, 1))
+            l2_M(oi, 0, 512, (0, 1), 5)
         for n in range(2, 4):
             w_W("w2", n)
         operand_run(w2_units[4:8], ("act",), 2)
@@ -390,23 +389,27 @@ def tile_autoregressiveresidualblock_kernel(
         for G in (0, 1, 3, 2):
             g_Q(G, 1)
 
-        def out_run(ois, h):
-            for oi in ois:
-                l2o_T(oi, h)
-                l2o_S(oi, h, ("dve", "act")[oi % 2])
-
         for oi in range(4):
-            l2o_M(oi, 0, (2, 3, 4, 5))
-            l2o_E(oi, 0)
-            l2o_A(oi, 0)
-        for oi in range(4):
-            l2o_M(oi, 1, (0, 1))
-        for oi in range(4):
-            l2o_M(oi, 1, (2, 3, 5, 4))
-            l2o_E(oi, 1)
-            l2o_A(oi, 1)
-            if oi == 1:
-                out_run((0, 1), 0)
-            if oi == 2:
-                out_run((2, 3), 0)
-        out_run((0, 1, 2, 3), 1)
+            l2_M(oi, 0, 512, (2, 3, 4, 5), 5)
+            l2_E(oi, 0, 512)
+        for oi in range(3):
+            l2_M(oi, 512, 512, (0, 1), 4)
+        l2_M(0, 512, 512, (2, 3, 5, 4), 4)
+        l2_E(0, 512, 512)
+        l2_M(1, 512, 512, (2, 3, 5, 4), 4)
+        l2_E(1, 512, 512)
+        l2_T(0, 0, 512, "dve")
+        l2_T(1, 0, 512, "act")
+        l2_M(2, 512, 512, (2, 3, 5, 4), 4)
+        l2_E(2, 512, 512)
+        l2_T(2, 0, 512, "dve")
+        l2_T(3, 0, 512, "act")
+        l2_M(3, 512, 256, (0, 1, 2, 3, 5, 4), 4)
+        l2_E(3, 512, 256)
+        l2_T(0, 512, 512, "dve")
+        l2_M(3, 768, 256, (0, 1, 2, 3, 5, 4), 4)
+        l2_E(3, 768, 256)
+        l2_T(1, 512, 512, "act")
+        l2_T(2, 512, 512, "dve")
+        l2_T(3, 512, 256, "act")
+        l2_T(3, 768, 256, "dve")

@@ -33,8 +33,7 @@ def tile_autoregressiveresidualblock_kernel(
         gg_pool = ctx.enter_context(tc.tile_pool(name="gg", bufs=5))
         v_pool = ctx.enter_context(tc.tile_pool(name="vpool", bufs=8))
         o_pool = ctx.enter_context(tc.tile_pool(name="opool", bufs=4))
-        ps_t = ctx.enter_context(tc.psum_pool(name="pst", bufs=4))
-        ps_a = ctx.enter_context(tc.psum_pool(name="psa", bufs=4))
+        psum = ctx.enter_context(tc.psum_pool(name="psum", bufs=8))
 
         live = {}
 
@@ -97,7 +96,7 @@ def tile_autoregressiveresidualblock_kernel(
 
         def load_rows2():
             for n, vec in enumerate((b2, bn2_scale, bn2_bias, bn2_mean, bn2_var, b_skip)):
-                nc.scalar.dma_start(out=rows2[4 * n:4 * n + 4, :], in_=vec.rearrange("(i p) -> i p", p=P))
+                nc.sync.dma_start(out=rows2[4 * n:4 * n + 4, :], in_=vec.rearrange("(i p) -> i p", p=P))
 
         def load_w2():
             for pr in range(2):
@@ -119,28 +118,15 @@ def tile_autoregressiveresidualblock_kernel(
             "w2": (w2_c, w2_s),
         }
 
-        vt = const.tile([P, 5, 12], F32, name="vt", tag="vt")
-        skip = const.tile([P, 4], F32, name="skip", tag="skip")
-        gain = const.tile([P, 12], F32, name="gain", tag="gain")
-        shift = const.tile([P, 12], F32, name="shift", tag="shift")
-        bias = const.tile([P, 12], F32, name="bias", tag="bias")
-        pos = const.tile([P, 12], F32, name="pos", tag="pos")
-        neg = const.tile([P, 12], F32, name="neg", tag="neg")
-        lo = const.tile([P, 12], F32, name="lo", tag="lo")
-        hi = const.tile([P, 12], F32, name="hi", tag="hi")
+        def channel_tiles(k, vectors, n):
+            names = ("gain", "shift", "bias", "pos", "neg", "lo", "hi")
+            vt = const.tile([P, vectors, n], F32, name=f"vt{k}", tag=f"vt{k}")
+            return [vt] + [const.tile([P, n], F32, name=f"{nm}{k}", tag=f"{nm}{k}") for nm in names]
 
-        def prep_bn():
-            tp = ps_t.tile([P, 3, P], BF16, name="tp", tag="tp")
-            for e in range(2):
-                nc.tensor.transpose(tp[:, e, :], rows1[:, e:2 * P:2], ident_b[:])
-            nc.tensor.transpose(tp[:, 2, :], rows2[:], ident_b[:])
-            nc.vector.tensor_copy(
-                out=vt[:, :, 0:8].rearrange("p n (g e) -> p e n g", e=2),
-                in_=tp[:, 0:2, 0:20].rearrange("p e (n g) -> p e n g", g=4),
-            )
-            nc.vector.tensor_copy(out=vt[:, :, 8:12], in_=tp[:, 2, 0:20].rearrange("p (n i) -> p n i", i=4))
-            nc.vector.tensor_copy(out=skip[:], in_=tp[:, 2, 20:24])
-            nc.vector.tensor_add(out=vt[:, 0, 8:12], in0=vt[:, 0, 8:12], in1=skip[:])
+        vt1, gain1, shift1, bias1, pos1, neg1, lo1, hi1 = channel_tiles(1, 5, 8)
+        vt2, gain2, shift2, bias2, pos2, neg2, lo2, hi2 = channel_tiles(2, 6, 4)
+
+        def constants(vt, gain, shift, bias, pos, neg, lo, hi):
             nc.vector.tensor_scalar_add(out=gain[:], in0=vt[:, 4, :], scalar1=EPS)
             nc.scalar.activation(out=gain[:], in_=gain[:], func=ACTF.Sqrt)
             nc.vector.reciprocal(out=gain[:], in_=gain[:])
@@ -154,8 +140,25 @@ def tile_autoregressiveresidualblock_kernel(
             nc.vector.scalar_tensor_tensor(out=lo[:], in0=neg[:], scalar=BIG, in1=shift[:], op0=ALU.mult, op1=ALU.add)
             nc.vector.scalar_tensor_tensor(out=hi[:], in0=pos[:], scalar=BIG, in1=shift[:], op0=ALU.mult, op1=ALU.add)
 
+        def prep_bn1():
+            tp = psum.tile([P, 2, P], BF16, name="tp", tag="bank")
+            for e in range(2):
+                nc.tensor.transpose(tp[:, e, :], rows1[:, e:2 * P:2], ident_b[:])
+            nc.vector.tensor_copy(
+                out=vt1[:].rearrange("p n (g e) -> p e n g", e=2),
+                in_=tp[:, :, 0:20].rearrange("p e (n g) -> p e n g", g=4),
+            )
+            constants(vt1, gain1, shift1, bias1, pos1, neg1, lo1, hi1)
+
+        def prep_bn2():
+            tp = psum.tile([P, P], BF16, name="tp", tag="bank")
+            nc.tensor.transpose(tp[:], rows2[:], ident_b[:])
+            nc.vector.tensor_copy(out=vt2[:], in_=tp[:, 0:24].rearrange("p (n i) -> p n i", i=4))
+            nc.vector.tensor_add(out=vt2[:, 0, :], in0=vt2[:, 0, :], in1=vt2[:, 5, :])
+            constants(vt2, gain2, shift2, bias2, pos2, neg2, lo2, hi2)
+
         def a_T(g, jj):
-            tp = ps_t.tile([P, 1024], BF16, name="tp", tag="tp")
+            tp = psum.tile([P, 1024], BF16, name="tp", tag="bank")
             for u in range(2):
                 for blk in range(4):
                     c0 = 512 * u + P * blk
@@ -195,7 +198,7 @@ def tile_autoregressiveresidualblock_kernel(
             return live["wW", "w2", 2 * j + ii][:, c0:c0 + P]
 
         def w_T(nm, g, j):
-            tp = ps_t.tile([P, 2, 256], F32, name="tp", tag="tp")
+            tp = psum.tile([P, 2, 256], F32, name="tp", tag="bank")
             for ii in range(2):
                 for u in range(2):
                     nc.tensor.transpose(tp[:, u, P * ii:P * ii + P], w_src(nm, g, j, ii, u), ident_f[:])
@@ -216,7 +219,7 @@ def tile_autoregressiveresidualblock_kernel(
             return live["S", G, h]
 
         def q_T(G, h):
-            tp = ps_t.tile([P, 2, 512], BF16, name="tp", tag="tp")
+            tp = psum.tile([P, 2, 512], BF16, name="tp", tag="bank")
             for u in range(2):
                 for tt in range(4):
                     nc.tensor.transpose(tp[:, u, P * tt:P * tt + P], q2_t[:, 4 * h + tt, 256 * G + u:256 * G + 256:2], ident_b[:])
@@ -226,7 +229,7 @@ def tile_autoregressiveresidualblock_kernel(
             evac(eng, s_tile(G, h)[:, 0:4:2, :], live["qT", G, h][:])
 
         def l1_M(i, h):
-            acc = ps_a.tile([P, 512], F32, name="acc", tag="acc")
+            acc = psum.tile([P, 512], F32, name="acc", tag="bank")
             for g in range(2):
                 nc.tensor.matmul_mx(
                     out=acc[:],
@@ -238,13 +241,13 @@ def tile_autoregressiveresidualblock_kernel(
 
         def l1_E(i, h):
             v = v_pool.tile([P, 512], BF16, name="vlin", tag="vlin")
-            nc.scalar.activation(out=v[:], in_=live["l1", i, h][:], func=ACTF.Identity, bias=bias[:, i:i + 1], scale=gain[:, i:i + 1])
+            nc.scalar.activation(out=v[:], in_=live["l1", i, h][:], func=ACTF.Identity, bias=bias1[:, i:i + 1], scale=gain1[:, i:i + 1])
             live["v", i, h] = v
 
         def l1_A(i, h):
             nc.vector.tensor_scalar(
                 out=s_tile(i // 2, h)[:, 2 * (i % 2) + 1, :], in0=live["v", i, h][:],
-                scalar1=lo[:, i:i + 1], scalar2=hi[:, i:i + 1], op0=ALU.max, op1=ALU.min,
+                scalar1=lo1[:, i:i + 1], scalar2=hi1[:, i:i + 1], op0=ALU.max, op1=ALU.min,
             )
 
         def g_R(G, h, eng="dve"):
@@ -260,7 +263,7 @@ def tile_autoregressiveresidualblock_kernel(
 
         def l2_M(oi, c0, w, parts, stop):
             if ("l2", oi, c0) not in live:
-                live["l2", oi, c0] = ps_a.tile([P, w], F32, name="acc", tag="acc")
+                live["l2", oi, c0] = psum.tile([P, w], F32, name="acc", tag="bank")
             acc = live["l2", oi, c0]
             rows = slice(P * oi, P * oi + P)
             cols = slice(c0, c0 + w)
@@ -278,14 +281,14 @@ def tile_autoregressiveresidualblock_kernel(
 
         def l2_E(oi, c0, w):
             v = o_pool.tile([P, w], F32, name="olin", tag="olin")
-            nc.scalar.activation(out=v[:], in_=live["l2", oi, c0][:], func=ACTF.Identity, bias=bias[:, 8 + oi:9 + oi], scale=gain[:, 8 + oi:9 + oi])
+            nc.scalar.activation(out=v[:], in_=live["l2", oi, c0][:], func=ACTF.Identity, bias=bias2[:, oi:oi + 1], scale=gain2[:, oi:oi + 1])
             y = o_pool.tile([P, w], F32, name="ocl", tag="ocl", align_bytes=64)
-            nc.vector.tensor_scalar(out=y[:], in0=v[:], scalar1=lo[:, 8 + oi:9 + oi], scalar2=hi[:, 8 + oi:9 + oi], op0=ALU.max, op1=ALU.min)
+            nc.vector.tensor_scalar(out=y[:], in0=v[:], scalar1=lo2[:, oi:oi + 1], scalar2=hi2[:, oi:oi + 1], op0=ALU.max, op1=ALU.min)
             live["oy", oi, c0] = y
 
         def l2_T(oi, c0, w, eng):
             t0, nt = c0 // P, w // P
-            tp = ps_t.tile([P, nt, P], F32, name="tp", tag="tp")
+            tp = psum.tile([P, nt, P], F32, name="tp", tag="bank")
             for tt in range(nt):
                 nc.tensor.transpose(tp[:, tt, :], live["oy", oi, c0][:, P * tt:P * tt + P], ident_f[:])
             yt = o_pool.tile([P, nt, P], F32, name="otr", tag="otr", bufs=6)
@@ -329,6 +332,7 @@ def tile_autoregressiveresidualblock_kernel(
         load_a(1)
         load_w1((1, 2, 3))
         load_a(2)
+        load_rows2()
         load_ws()
         load_q2(0)
         load_w2()
@@ -349,22 +353,22 @@ def tile_autoregressiveresidualblock_kernel(
                     l1_A(i, h)
 
         def idle_run(n):
-            idle = ps_t.tile([P, 512], F32, name="tp", tag="tp")
+            idle = psum.tile([P, 512], F32, name="tp", tag="bank")
             for k in range(n):
                 nc.tensor.matmul(idle[:], lhsT=zeros[:, 0:P], rhs=zeros[:], start=True, stop=True)
 
         idle_run(5)
         operand_run(a_units[0:2] + w1_units[0:2], ("dve", "act", "act"), 2)
+        prep_bn1()
         idle_run(2)
         operand_run(a_units[2:4] + w1_units[2:4], ("act", "act", "dve"), 2)
-        load_rows2()
-        prep_bn()
         operand_run(w1_units[4:8], ("dve", "act", "act"), 2)
         l1_run(range(0, 4), 0)
         operand_run(a_units[4:8], ("act",), 2)
         for n in range(2):
             w_W("ws", n)
         operand_run(ws_units, ("act", "act", "dve"), 2)
+        prep_bn2()
         l1_run(range(4, 8), 0)
         queue_run(0, ("act",))
         l1_run(range(0, 8), 1)

@@ -332,9 +332,9 @@ def tile_autoregressiveresidualblock_kernel(
         load_a(1)
         load_w1((1, 2, 3))
         load_a(2)
-        load_rows2()
         load_ws()
         load_q2(0)
+        load_rows2()
         load_w2()
         load_q2(1)
 
@@ -368,9 +368,9 @@ def tile_autoregressiveresidualblock_kernel(
         for n in range(2):
             w_W("ws", n)
         operand_run(ws_units, ("act", "act", "dve"), 2)
-        prep_bn2()
         l1_run(range(4, 8), 0)
         queue_run(0, ("act",))
+        prep_bn2()
         l1_run(range(0, 8), 1)
         for n in range(2):
             w_W("w2", n)

@@ -367,19 +367,22 @@ def tile_autoregressiveresidualblock_kernel(
         operand_run(a_units[4:8], ("act",), 2)
         for n in range(2):
             w_W("ws", n)
+        l1_run(range(4, 6), 0)
         operand_run(ws_units, ("act", "act", "dve"), 2)
-        l1_run(range(4, 8), 0)
+        l1_run(range(6, 8), 0)
         queue_run(0, ("act",))
         prep_bn2()
         l1_run(range(0, 8), 1)
         for n in range(2):
             w_W("w2", n)
         operand_run(w2_units[0:4], ("act",), 2)
-        for oi in range(4):
+        for oi in range(2):
             l2_M(oi, 0, 512, (0, 1), 5)
         for n in range(2, 4):
             w_W("w2", n)
         operand_run(w2_units[4:8], ("act",), 2)
+        for oi in range(2, 4):
+            l2_M(oi, 0, 512, (0, 1), 5)
         for G in range(4):
             g_R(G, 0)
         for G in range(4):
@@ -396,18 +399,16 @@ def tile_autoregressiveresidualblock_kernel(
         for oi in range(4):
             l2_M(oi, 0, 512, (2, 3, 4, 5), 5)
             l2_E(oi, 0, 512)
-        for oi in range(3):
-            l2_M(oi, 512, 512, (0, 1), 4)
-        l2_M(0, 512, 512, (2, 3, 5, 4), 4)
-        l2_E(0, 512, 512)
-        l2_M(1, 512, 512, (2, 3, 5, 4), 4)
-        l2_E(1, 512, 512)
-        l2_T(0, 0, 512, "dve")
-        l2_T(1, 0, 512, "act")
-        l2_M(2, 512, 512, (2, 3, 5, 4), 4)
+        for parts in ((0, 1), (2,), (3,)):
+            for oi in range(3):
+                l2_M(oi, 512, 512, parts, 4)
+        for oi in range(2):
+            l2_M(oi, 512, 512, (5, 4), 4)
+            l2_E(oi, 512, 512)
+        for oi in range(4):
+            l2_T(oi, 0, 512, ("dve", "act")[oi % 2])
+        l2_M(2, 512, 512, (5, 4), 4)
         l2_E(2, 512, 512)
-        l2_T(2, 0, 512, "dve")
-        l2_T(3, 0, 512, "act")
         l2_M(3, 512, 256, (0, 1, 2, 3, 5, 4), 4)
         l2_E(3, 512, 256)
         l2_T(0, 512, 512, "dve")

from contextlib import ExitStack

import concourse.mybir as mybir
from concourse.masks import make_identity

F32 = mybir.dt.float32
BF16 = mybir.dt.bfloat16
U32 = mybir.dt.uint32
U8 = mybir.dt.uint8
FP8X4 = mybir.dt.float8_e4m3fn_x4
ALU = mybir.AluOpType
ACTF = mybir.ActivationFunctionType

P = 128
BS, DIN, MID, OUT = 1024, 512, 1024, 512
EPS = 1e-5
BIG = 3.0e38
FLOPS = 2 * BS * (2 * DIN * MID + 2 * MID * OUT + 2 * DIN * OUT)
BYTES = 2 * (2 * BS * DIN + BS * MID + 2 * DIN * MID + 2 * MID * OUT + 2 * DIN * OUT) + 4 * BS * OUT


def tile_autoregressiveresidualblock_kernel(
    tc, x, conv1_queue, conv2_queue, w1, b1, w2, b2, w_skip, b_skip,
    bn1_scale, bn1_bias, bn1_mean, bn1_var, bn2_scale, bn2_bias, bn2_mean, bn2_var, out,
):
    nc = tc.nc
    with ExitStack() as ctx:
        const = ctx.enter_context(tc.tile_pool(name="const", bufs=1))
        raw = ctx.enter_context(tc.tile_pool(name="raw", bufs=1))
        keep = ctx.enter_context(tc.tile_pool(name="keep", bufs=1))
        grp_pool = ctx.enter_context(tc.tile_pool(name="grp", bufs=8))
        s_pool = ctx.enter_context(tc.tile_pool(name="spool", bufs=8))
        gg_pool = ctx.enter_context(tc.tile_pool(name="gg", bufs=5))
        v_pool = ctx.enter_context(tc.tile_pool(name="vpool", bufs=8))
        o_pool = ctx.enter_context(tc.tile_pool(name="opool", bufs=4))
        psum = ctx.enter_context(tc.psum_pool(name="psum", bufs=8))

        live = {}

        def evac(eng, dst, src):
            if eng == "act":
                nc.scalar.copy(out=dst, in_=src)
            else:
                nc.vector.tensor_copy(out=dst, in_=src)

        rows1 = const.tile([P, 2 * P], BF16, name="rows1", tag="rows1")
        rows2 = const.tile([P, P], BF16, name="rows2", tag="rows2")
        zeros = const.tile([P, 512], BF16, name="zeros", tag="zeros")
        nc.vector.memset(zeros[:], 0.0)
        nc.vector.memset(rows1[:], 0.0)
        nc.vector.memset(rows2[:], 0.0)
        for n, vec in enumerate((b1, bn1_scale, bn1_bias, bn1_mean, bn1_var)):
            nc.scalar.dma_start(out=rows1[4 * n:4 * n + 4, :], in_=vec.rearrange("(i p) -> i p", p=2 * P))
        ident_b = const.tile([P, P], BF16, name="ident_b", tag="ident_b")
        nc.vector.memset(ident_b[:], 0.0)
        make_identity(nc, ident_b[:], nomemset=True)
        ident_f = const.tile([P, P], F32, name="ident_f", tag="ident_f")
        nc.vector.tensor_copy(out=ident_f[:], in_=ident_b[:])
        warm = const.tile([P, 1], F32, name="warm", tag="warm")
        nc.vector.memset(warm[:], 1.0)
        nc.scalar.activation(out=warm[:], in_=warm[:], func=ACTF.Sqrt)

        a_chunks = ((0, 2), (2, 2), (4, 4))
        a_sb = [raw.tile([P, 2, nt, DIN], BF16, name=f"a_sb{t0}", tag=f"a_sb{t0}") for t0, nt in a_chunks]
        q2_sb = raw.tile([P, 8 * MID], BF16, name="q2_sb", tag="q2_sb")
        w1_sb = [raw.tile([P, 4 * DIN], BF16, name=f"w1_sb{j}", tag=f"w1_sb{j}") for j in range(4)]
        ws_sb = raw.tile([P, 4 * 2 * DIN], BF16, name="ws_sb", tag="ws_sb")
        w2_sb = raw.tile([P, 4 * 2 * MID], BF16, name="w2_sb", tag="w2_sb")
        a_of = {t0 + k: (tile, k) for (t0, nt), tile in zip(a_chunks, a_sb) for k in range(nt)}
        taps = (
            conv1_queue[0].rearrange("(e j t) c o -> j e t (c o)", e=2, t=8),
            x.rearrange("(e j t) c o -> j e t (c o)", e=2, t=8),
        )
        q2_v = conv2_queue[0].rearrange("(p t) c o -> p t (c o)", t=8)
        q2_t = q2_sb[:].rearrange("p (t c) -> p t c", t=8)
        w1_v = w1.rearrange("(g p e) k -> p g (e k)", p=P, e=2)
        ws_v = w_skip.rearrange("(i p) k -> p i k", p=P)
        w2_v = w2.rearrange("(i p) k -> p i k", p=P)
        ws_t = ws_sb[:].rearrange("p (i k) -> p i k", i=4)
        w2_t = w2_sb[:].rearrange("p (i k) -> p i k", i=4)

        def load_a(n):
            t0, nt = a_chunks[n]
            for tap in range(2):
                nc.sync.dma_start(out=a_sb[n][tap:P:2, :, :, :], in_=taps[tap][:, :, t0:t0 + nt, :])

        def load_w1(prs):
            for pr in prs:
                nc.sync.dma_start(out=w1_sb[pr][:], in_=w1_v[:, pr, :])

        def load_q2(h):
            nc.sync.dma_start(out=q2_t[:, 4 * h:4 * h + 4, :], in_=q2_v[:, 4 * h:4 * h + 4, :])

        def load_ws():
            nc.sync.dma_start(out=ws_t, in_=ws_v)

        def load_rows2():
            for n, vec in enumerate((b2, bn2_scale, bn2_bias, bn2_mean, bn2_var, b_skip)):
                nc.sync.dma_start(out=rows2[4 * n:4 * n + 4, :], in_=vec.rearrange("(i p) -> i p", p=P))

        def load_w2():
            for pr in range(2):
                nc.sync.dma_start(out=w2_t[:, 2 * pr:2 * pr + 2, :], in_=w2_v[:, 2 * pr:2 * pr + 2, :])

        a_c = keep.tile([P, 2, BS], U32, name="a_c", tag="a_c", align_bytes=64)
        a_s = keep.tile([P, 2, BS], U8, name="a_s", tag="a_s", align_bytes=64)
        g_c = keep.tile([P, 4, BS], U32, name="g_c", tag="g_c", align_bytes=64)
        g_s = keep.tile([P, 4, BS], U8, name="g_s", tag="g_s", align_bytes=64)
        w1_c = keep.tile([P, 2, MID], U32, name="w1_c", tag="w1_c", align_bytes=64)
        w1_s = keep.tile([P, 2, MID], U8, name="w1_s", tag="w1_s", align_bytes=64)
        ws_c = keep.tile([P, 2, OUT], U32, name="ws_c", tag="ws_c", align_bytes=64)
        ws_s = keep.tile([P, 2, OUT], U8, name="ws_s", tag="ws_s", align_bytes=64)
        w2_c = keep.tile([P, 4, OUT], U32, name="w2_c", tag="w2_c", align_bytes=64)
        w2_s = keep.tile([P, 4, OUT], U8, name="w2_s", tag="w2_s", align_bytes=64)
        weights = {
            "w1": (w1_c, w1_s),
            "ws": (ws_c, ws_s),
            "w2": (w2_c, w2_s),
        }

        def channel_tiles(k, vectors, n):
            names = ("gain", "shift", "bias", "pos", "neg", "lo", "hi")
            vt = const.tile([P, vectors, n], F32, name=f"vt{k}", tag=f"vt{k}")
            return [vt] + [const.tile([P, n], F32, name=f"{nm}{k}", tag=f"{nm}{k}") for nm in names]

        vt1, gain1, shift1, bias1, pos1, neg1, lo1, hi1 = channel_tiles(1, 5, 8)
        vt2, gain2, shift2, bias2, pos2, neg2, lo2, hi2 = channel_tiles(2, 6, 4)

        def constants(vt, gain, shift, bias, pos, neg, lo, hi):
            nc.vector.tensor_scalar_add(out=gain[:], in0=vt[:, 4, :], scalar1=EPS)
            nc.scalar.activation(out=gain[:], in_=gain[:], func=ACTF.Sqrt)
            nc.vector.reciprocal(out=gain[:], in_=gain[:])
            nc.vector.tensor_mul(out=gain[:], in0=vt[:, 1, :], in1=gain[:])
            nc.vector.tensor_mul(out=shift[:], in0=vt[:, 3, :], in1=gain[:])
            nc.vector.tensor_sub(out=shift[:], in0=vt[:, 2, :], in1=shift[:])
            nc.vector.tensor_mul(out=bias[:], in0=vt[:, 0, :], in1=gain[:])
            nc.vector.tensor_add(out=bias[:], in0=bias[:], in1=shift[:])
            nc.vector.tensor_scalar(out=pos[:], in0=gain[:], scalar1=0.0, scalar2=None, op0=ALU.is_ge)
            nc.vector.tensor_scalar(out=neg[:], in0=pos[:], scalar1=-1.0, scalar2=None, op0=ALU.add)
            nc.vector.scalar_tensor_tensor(out=lo[:], in0=neg[:], scalar=BIG, in1=shift[:], op0=ALU.mult, op1=ALU.add)
            nc.vector.scalar_tensor_tensor(out=hi[:], in0=pos[:], scalar=BIG, in1=shift[:], op0=ALU.mult, op1=ALU.add)

        def prep_bn1():
            tp = psum.tile([P, 2, P], BF16, name="tp", tag="bank")
            for e in range(2):
                nc.tensor.transpose(tp[:, e, :], rows1[:, e:2 * P:2], ident_b[:])
            nc.vector.tensor_copy(
                out=vt1[:].rearrange("p n (g e) -> p e n g", e=2),
                in_=tp[:, :, 0:20].rearrange("p e (n g) -> p e n g", g=4),
            )
            constants(vt1, gain1, shift1, bias1, pos1, neg1, lo1, hi1)

        def prep_bn2():
            tp = psum.tile([P, P], BF16, name="tp", tag="bank")
            nc.tensor.transpose(tp[:], rows2[:], ident_b[:])
            nc.vector.tensor_copy(out=vt2[:], in_=tp[:, 0:24].rearrange("p (n i) -> p n i", i=4))
            nc.vector.tensor_add(out=vt2[:, 0, :], in0=vt2[:, 0, :], in1=vt2[:, 5, :])
            constants(vt2, gain2, shift2, bias2, pos2, neg2, lo2, hi2)

        def a_T(g, jj):
            tp = psum.tile([P, 1024], BF16, name="tp", tag="bank")
            for u in range(2):
                for blk in range(4):
                    c0 = 512 * u + P * blk
                    src, t = a_of[2 * jj + blk // 2]
                    nc.tensor.transpose(tp[:, c0:c0 + P], src[:, blk % 2, t, 256 * g + u:256 * g + 256:2], ident_b[:])
            live["aT", g, jj] = tp

        def a_C(g, jj, eng):
            grp = grp_pool.tile([P, 1024], BF16, name="grp", tag="grp", align_bytes=64)
            evac(eng, grp[:].bitcast(F32).rearrange("p (n u) -> p n u", u=2),
                 live["aT", g, jj][:].bitcast(F32).rearrange("p (u n) -> p n u", u=2))
            live["aC", g, jj] = grp

        def a_Q(g, jj):
            cols = slice(256 * jj, 256 * jj + 256)
            nc.vector.quantize_mx(out=a_c[:, g, cols].bitcast(FP8X4), scales=a_s[:, g, cols], in_=live["aC", g, jj][:])

        sorted_tags = {"ws": ("a_sb0", "a_sb2"), "w2": ("w1_sb0", "w1_sb1", "w1_sb2", "w1_sb3")}

        def w_W(nm, n):
            src = {"ws": ws_sb, "w2": w2_sb}[nm]
            dst = raw.tile([P, 1024], F32, name="wsort", tag=sorted_tags[nm][n])
            nc.vector.tensor_copy(
                out=dst[:].rearrange("p (x u q) -> p x u q", u=2, q=P),
                in_=src[:].bitcast(F32)[:, 1024 * n:1024 * n + 1024].rearrange("p (x q u) -> p x u q", u=2, q=P),
            )
            live["wW", nm, n] = dst

        def w_src(nm, g, j, ii, u):
            if nm == "w1":
                c0 = 512 * ii + 256 * g
                return w1_sb[j][:].bitcast(F32)[:, c0 + u:c0 + 256:2]
            if nm == "ws":
                c0 = P * ((2 * ii + g) * 2 + u)
                return live["wW", "ws", j][:, c0:c0 + P]
            c0 = P * (2 * g + u)
            return live["wW", "w2", 2 * j + ii][:, c0:c0 + P]

        def w_T(nm, g, j):
            tp = psum.tile([P, 2, 256], F32, name="tp", tag="bank")
            for ii in range(2):
                for u in range(2):
                    nc.tensor.transpose(tp[:, u, P * ii:P * ii + P], w_src(nm, g, j, ii, u), ident_f[:])
            live["wT", nm, g, j] = tp

        def w_C(nm, g, j, eng):
            grp = grp_pool.tile([P, 1024], BF16, name="grp", tag="grp", align_bytes=64)
            evac(eng, grp[:].bitcast(F32).rearrange("p (r u) -> p r u", u=2), live["wT", nm, g, j][:].rearrange("p u r -> p r u"))
            live["wC", nm, g, j] = grp

        def w_Q(nm, g, j):
            cols = slice(256 * j, 256 * j + 256)
            nc.vector.quantize_mx(out=weights[nm][0][:, g, cols].bitcast(FP8X4), scales=weights[nm][1][:, g, cols], in_=live["wC", nm, g, j][:])

        def s_tile(G, h):
            if ("S", G, h) not in live:
                live["S", G, h] = s_pool.tile([P, 4, 512], BF16, name="stile", tag="stile")
            return live["S", G, h]

        def q_T(G, h):
            tp = psum.tile([P, 2, 512], BF16, name="tp", tag="bank")
            for u in range(2):
                for tt in range(4):
                    nc.tensor.transpose(tp[:, u, P * tt:P * tt + P], q2_t[:, 4 * h + tt, 256 * G + u:256 * G + 256:2], ident_b[:])
            live["qT", G, h] = tp

        def q_C(G, h, eng):
            evac(eng, s_tile(G, h)[:, 0:4:2, :], live["qT", G, h][:])

        def l1_M(i, h):
            acc = psum.tile([P, 512], F32, name="acc", tag="bank")
            for g in range(2):
                nc.tensor.matmul_mx(
                    out=acc[:],
                    lhsT=w1_c[:, g, P * i:P * i + P].bitcast(FP8X4), lhsT_scale=w1_s[:, g, P * i:P * i + P],
                    rhs=a_c[:, g, 512 * h:512 * h + 512].bitcast(FP8X4), rhs_scale=a_s[:, g, 512 * h:512 * h + 512],
                    start=(g == 0), stop=(g == 1),
                )
            live["l1", i, h] = acc

        def l1_E(i, h):
            v = v_pool.tile([P, 512], BF16, name="vlin", tag="vlin")
            nc.scalar.activation(out=v[:], in_=live["l1", i, h][:], func=ACTF.Identity, bias=bias1[:, i:i + 1], scale=gain1[:, i:i + 1])
            live["v", i, h] = v

        def l1_A(i, h):
            nc.vector.tensor_scalar(
                out=s_tile(i // 2, h)[:, 2 * (i % 2) + 1, :], in0=live["v", i, h][:],
                scalar1=lo1[:, i:i + 1], scalar2=hi1[:, i:i + 1], op0=ALU.max, op1=ALU.min,
            )

        def g_R(G, h, eng="dve"):
            gg = gg_pool.tile([P, 2048], BF16, name="ggt", tag="ggt", align_bytes=64)
            evac(eng, gg[:].rearrange("p (c i t) -> p c t i", i=4, t=4), live["S", G, h][:].rearrange("p t (c i) -> p c t i", i=4))
            live["gg", G, h] = gg

        def g_Q(G, h):
            cols = slice(512 * h, 512 * h + 512)
            nc.vector.quantize_mx(out=g_c[:, G, cols].bitcast(FP8X4), scales=g_s[:, G, cols], in_=live["gg", G, h][:])

        out_r = out.rearrange("(m t) c o -> m t (c o)", t=8)

        def l2_M(oi, c0, w, parts, stop):
            if ("l2", oi, c0) not in live:
                live["l2", oi, c0] = psum.tile([P, w], F32, name="acc", tag="bank")
            acc = live["l2", oi, c0]
            rows = slice(P * oi, P * oi + P)
            cols = slice(c0, c0 + w)
            for part in parts:
                if part < 2:
                    lc, ls, rc, rs, g = ws_c, ws_s, a_c, a_s, part
                else:
                    lc, ls, rc, rs, g = w2_c, w2_s, g_c, g_s, part - 2
                nc.tensor.matmul_mx(
                    out=acc[:],
                    lhsT=lc[:, g, rows].bitcast(FP8X4), lhsT_scale=ls[:, g, rows],
                    rhs=rc[:, g, cols].bitcast(FP8X4), rhs_scale=rs[:, g, cols],
                    start=(part == 0), stop=(part == stop),
                )

        def l2_E(oi, c0, w):
            v = o_pool.tile([P, w], F32, name="olin", tag="olin")
            nc.scalar.activation(out=v[:], in_=live["l2", oi, c0][:], func=ACTF.Identity, bias=bias2[:, oi:oi + 1], scale=gain2[:, oi:oi + 1])
            y = o_pool.tile([P, w], F32, name="ocl", tag="ocl", align_bytes=64)
            nc.vector.tensor_scalar(out=y[:], in0=v[:], scalar1=lo2[:, oi:oi + 1], scalar2=hi2[:, oi:oi + 1], op0=ALU.max, op1=ALU.min)
            live["oy", oi, c0] = y

        def l2_T(oi, c0, w, eng):
            t0, nt = c0 // P, w // P
            tp = psum.tile([P, nt, P], F32, name="tp", tag="bank")
            for tt in range(nt):
                nc.tensor.transpose(tp[:, tt, :], live["oy", oi, c0][:, P * tt:P * tt + P], ident_f[:])
            yt = o_pool.tile([P, nt, P], F32, name="otr", tag="otr", bufs=6)
            evac(eng, yt[:], tp[:])
            nc.sync.dma_start(out=out_r[:, t0:t0 + nt, P * oi:P * oi + P], in_=yt[:])

        def T(u):
            if u[0] == "a":
                a_T(u[1], u[2])
            else:
                w_T(u[0], u[1], u[2])

        def C(u, eng):
            if u[0] == "a":
                a_C(u[1], u[2], eng)
            else:
                w_C(u[0], u[1], u[2], eng)

        def Q(u):
            if u[0] == "a":
                a_Q(u[1], u[2])
            else:
                w_Q(u[0], u[1], u[2])

        def operand_run(units, engs, lag):
            for k, u in enumerate(units):
                T(u)
                C(u, engs[k % len(engs)])
                if k >= lag:
                    Q(units[k - lag])
            for u in units[len(units) - lag:]:
                Q(u)

        def queue_run(h, engs):
            for G in range(4):
                q_T(G, h)
                q_C(G, h, engs[G % len(engs)])

        load_a(0)
        load_w1((0,))
        load_a(1)
        load_w1((1, 2, 3))
        load_a(2)
        load_ws()
        load_q2(0)
        load_rows2()
        load_w2()
        load_q2(1)

        ctx.enter_context(tc.manual_schedule(engines={mybir.EngineType.PE}))

        a_units = [("a", g, j) for j in range(4) for g in range(2)]
        w1_units = [("w1", g, j) for j in range(4) for g in range(2)]
        ws_units = [("ws", g, j) for j in range(2) for g in range(2)]
        w2_units = [("w2", g, j) for j in range(2) for g in range(4)]

        def l1_run(ms, h):
            for i in ms:
                l1_M(i, h)
                l1_E(i, h)
                if h == 0:
                    l1_A(i, h)

        def idle_run(n):
            idle = psum.tile([P, 512], F32, name="tp", tag="bank")
            for k in range(n):
                nc.tensor.matmul(idle[:], lhsT=zeros[:, 0:P], rhs=zeros[:], start=True, stop=True)

        idle_run(5)
        operand_run(a_units[0:2] + w1_units[0:2], ("dve", "act", "act"), 2)
        prep_bn1()
        idle_run(2)
        operand_run(a_units[2:4] + w1_units[2:4], ("act", "act", "dve"), 2)
        operand_run(w1_units[4:8], ("dve", "act", "act"), 2)
        l1_run(range(0, 4), 0)
        operand_run(a_units[4:8], ("act",), 2)
        for n in range(2):
            w_W("ws", n)
        l1_run(range(4, 6), 0)
        operand_run(ws_units, ("act", "act", "dve"), 2)
        l1_run(range(6, 8), 0)
        queue_run(0, ("act",))
        prep_bn2()
        l1_run(range(0, 8), 1)
        for n in range(2):
            w_W("w2", n)
        operand_run(w2_units[0:4], ("act",), 2)
        for oi in range(2):
            l2_M(oi, 0, 512, (0, 1), 5)
        for n in range(2, 4):
            w_W("w2", n)
        operand_run(w2_units[4:8], ("act",), 2)
        for oi in range(2, 4):
            l2_M(oi, 0, 512, (0, 1), 5)
        for G in range(4):
            g_R(G, 0)
        for G in range(4):
            g_Q(G, 0)
        queue_run(1, ("act", "act", "dve"))
        for i in range(8):
            l1_A(i, 1)
        g_R(2, 1, "act")
        for G in (0, 1, 3):
            g_R(G, 1)
        for G in (0, 1, 3, 2):
            g_Q(G, 1)

        for oi in range(4):
            l2_M(oi, 0, 512, (2, 3, 4, 5), 5)
            l2_E(oi, 0, 512)
        for parts in ((0, 1), (2,), (3,)):
            for oi in range(3):
                l2_M(oi, 512, 512, parts, 4)
        for oi in range(2):
            l2_M(oi, 512, 512, (5, 4), 4)
            l2_E(oi, 512, 512)
        for oi in range(4):
            l2_T(oi, 0, 512, ("dve", "act")[oi % 2])
        l2_M(2, 512, 512, (5, 4), 4)
        l2_E(2, 512, 512)
        l2_M(3, 512, 256, (0, 1, 2, 3, 5, 4), 4)
        l2_E(3, 512, 256)
        l2_T(0, 512, 512, "dve")
        l2_M(3, 768, 256, (0, 1, 2, 3, 5, 4), 4)
        l2_E(3, 768, 256)
        l2_T(1, 512, 512, "act")
        l2_T(2, 512, 512, "dve")
        l2_T(3, 512, 256, "act")
        l2_T(3, 768, 256, "dve")
